import numpy as np
import ml_dtypes


def mxq(x, axis, fmt="e4m3"):
    dtype, down = {"e4m3": (ml_dtypes.float8_e4m3fn, 7), "e5m2": (ml_dtypes.float8_e5m2, 14)}[fmt]
    v = np.moveaxis(np.asarray(x, np.float32).astype(ml_dtypes.bfloat16).astype(np.float64), axis, -1)
    blocks = v.reshape(v.shape[:-1] + (-1, 32))
    amax = np.abs(blocks).max(-1, keepdims=True)
    byte = np.maximum(np.where(amax > 0, np.frexp(amax)[1] - 1 + 127, 0) - down, 1)
    scale = np.exp2(byte - 127.0)
    codes = (blocks / scale).astype(np.float32).astype(dtype).astype(np.float64)
    return np.moveaxis((codes * scale).reshape(v.shape), -1, axis)


WIDE = False


def mx_kscale(k):
    if not WIDE:
        return np.ones(k)
    levels = np.array([10, -10, 5, -5, 0])
    a = np.random.permutation(np.resize(levels, k // 512 * 4)).reshape(k // 512, 4)
    idx = np.arange(k)
    return np.exp2(a[idx // 512, idx % 128 // 32])


BF16 = ml_dtypes.bfloat16


def bf(x):
    return np.asarray(x, np.float32).astype(BF16)


def f64(x):
    return np.asarray(x).astype(np.float64)


E2M1 = np.array([0.0, 0.5, 1.0, 1.5, 2.0, 3.0, 4.0, 6.0, -0.0, -0.5, -1.0, -1.5, -2.0, -3.0, -4.0, -6.0])


def pack_weight(w, fmt):
    k, n = w.shape
    w = f64(bf(w)).reshape(k // 32, 32, n)
    amax = np.abs(w).max(1)
    if fmt == "e4m3":
        byte = np.frexp(amax)[1] - 1 + 127 - 7
    else:
        mant, ex = np.frexp(amax / 6.0)
        byte = np.where(mant > 0.5, ex, ex - 1) + 127
    byte = np.clip(np.where(amax > 0, byte, 1), 1, 254)
    scaled = (w * np.exp2(127.0 - byte)[:, None, :]).reshape(k, n).astype(np.float32)
    by_word = np.ascontiguousarray(scaled.reshape(k // 512, 128, 4, n).transpose(0, 1, 3, 2))
    if fmt == "e4m3":
        words = by_word.astype(ml_dtypes.float8_e4m3fn).view(np.uint8)
    else:
        c = by_word.astype(ml_dtypes.float4_e2m1fn).view(np.uint8) & 0xF
        words = c[..., 0::2] | (c[..., 1::2] << 4)
    return np.ascontiguousarray(words), np.ascontiguousarray(byte.astype(np.uint8).reshape(k // 512, 16, n))


def unpack_weight(words, scales, fmt):
    g, p, n, _ = words.shape
    if fmt == "e4m3":
        vals = np.ascontiguousarray(words).view(ml_dtypes.float8_e4m3fn).astype(np.float64)
    else:
        nib = np.empty((g, p, n, 4), np.uint8)
        nib[..., 0::2] = words & 0xF
        nib[..., 1::2] = words >> 4
        vals = E2M1[nib]
    vals = vals * np.repeat(np.exp2(scales.astype(np.float64) - 127.0), 8, axis=1)[..., None]
    return vals.transpose(0, 1, 3, 2).reshape(g * 512, n)


B, S, HID, NH, DH = 4, 1024, 1024, 4, 64
DQ = NH * DH
FMT = "e4m3"


def setup_inputs():
    s = mx_kscale(HID)

    def w():
        return pack_weight(np.random.standard_normal((HID, DQ)) / np.sqrt(HID) / s[:, None], FMT)

    def b():
        return bf(np.random.standard_normal(DQ) * 0.3)

    x = bf(np.random.standard_normal((B, S, HID)) * s)
    reasoning_mask = bf(np.random.uniform(size=(B, S, 1, 1)))
    Wq_words, Wq_scales = w()
    bq = b()
    Wk_words, Wk_scales = w()
    bk = b()
    Wqr_words, Wqr_scales = w()
    bqr = b()
    Wkr_words, Wkr_scales = w()
    bkr = b()
    return {"x": x,
            "reasoning_mask": reasoning_mask,
            "Wq_words": Wq_words, "Wq_scales": Wq_scales, "bq": bq,
            "Wk_words": Wk_words, "Wk_scales": Wk_scales, "bk": bk,
            "Wqr_words": Wqr_words, "Wqr_scales": Wqr_scales, "bqr": bqr,
            "Wkr_words": Wkr_words, "Wkr_scales": Wkr_scales, "bkr": bkr}


def reference(x, reasoning_mask, Wq_words, Wq_scales, bq, Wk_words, Wk_scales, bk, Wqr_words, Wqr_scales, bqr, Wkr_words, Wkr_scales, bkr):
    xq = mxq(f64(x), 2, "e4m3")
    g = f64(reasoning_mask)

    def proj(words, scales, b):
        return ((xq @ unpack_weight(words, scales, FMT)) + f64(b)).reshape(B, S, NH, DH)

    q = proj(Wq_words, Wq_scales, bq)
    k = proj(Wk_words, Wk_scales, bk)
    q_r = proj(Wqr_words, Wqr_scales, bqr)
    k_r = proj(Wkr_words, Wkr_scales, bkr)
    q = q * (1.0 - g) + q_r * g
    k = k * (1.0 - g) + k_r * g
    return q, k

@@ -1,0 +1,197 @@
+from contextlib import ExitStack
+
+import concourse.mybir as mybir
+from concourse.masks import make_identity
+
+F32 = mybir.dt.float32
+BF16 = mybir.dt.bfloat16
+I32 = mybir.dt.int32
+U32 = mybir.dt.uint32
+U8 = mybir.dt.uint8
+FP8X4 = mybir.dt.float8_e4m3fn_x4
+MULT = mybir.AluOpType.mult
+ADD = mybir.AluOpType.add
+SUBTRACT = mybir.AluOpType.subtract
+COPY = mybir.ActivationFunctionType.Copy
+
+P = 128
+TOKENS = 4096
+HID = 1024
+FEAT = 256
+K_PASS = 512
+PASSES = HID // K_PASS
+BANK = 2 * FEAT
+TILES = TOKENS // P
+GROUP = 4
+GROUPS = TILES // GROUP
+LOOKAHEAD = 3
+
+FLOPS = 2 * TOKENS * HID * 4 * FEAT
+
+
+def tile_reasoningmultiheadattention_pa_t_kernel(
+    tc, x, reasoning_mask,
+    Wq_words, Wq_scales, bq, Wk_words, Wk_scales, bk,
+    Wqr_words, Wqr_scales, bqr, Wkr_words, Wkr_scales, bkr,
+    out_0, out_1,
+):
+    nc = tc.nc
+    x_view = x.rearrange("b s k -> (b s) k").rearrange("(p t) k -> p t k", t=TILES)
+    m_view = reasoning_mask.rearrange("b s o i -> (b s o i)").rearrange("(p t) -> p t", t=TILES)
+    out_views = [
+        o.rearrange("b s h d -> (b s) (h d)").rearrange("(p t) n -> p t n", t=TILES) for o in (out_0, out_1)
+    ]
+    words_in = [[Wq_words, Wk_words], [Wqr_words, Wkr_words]]
+    scales_in = [[Wq_scales, Wk_scales], [Wqr_scales, Wkr_scales]]
+    bias_in = [[bq, bk], [bqr, bkr]]
+
+    with ExitStack() as ctx:
+        ctx.enter_context(tc.manual_schedule())
+        keep = ctx.enter_context(tc.tile_pool(name="keep", bufs=1))
+        stage = ctx.enter_context(tc.tile_pool(name="stage", bufs=6))
+        ahead = ctx.enter_context(tc.tile_pool(name="ahead", bufs=(LOOKAHEAD + 1) * GROUP))
+        psum_t = ctx.enter_context(tc.psum_pool(name="psum_t", bufs=4))
+        psum_mm = ctx.enter_context(tc.psum_pool(name="psum_mm", bufs=2))
+
+        ident = keep.tile([P, P], F32, name="ident")
+        make_identity(nc, ident[:])
+        ones = keep.tile([P, P], BF16, name="ones")
+        nc.vector.memset(ones[:], 1.0)
+        bias_rows = keep.tile([P, 2, BANK], BF16, name="bias_rows")
+        nc.vector.memset(bias_rows[:], 0.0)
+        w_planes = keep.tile([P, BANK], U8, name="w_planes", align_bytes=64)
+        nc.vector.memset(w_planes[:].bitcast(I32), 0)
+        for side in range(2):
+            for half in range(2):
+                nc.scalar.dma_start(
+                    out=bias_rows[0:1, side, half * FEAT : (half + 1) * FEAT],
+                    in_=bias_in[side][half].unsqueeze(0),
+                )
+        m_bf = keep.tile([P, TILES], BF16, name="m_bf")
+        nc.scalar.dma_start(out=m_bf[:], in_=m_view)
+
+        x_sb = [keep.tile([P, GROUP, HID], BF16, name="x%d" % i) for i in range(GROUPS)]
+        w_words = keep.tile([P, PASSES, 2, BANK], U32, name="w_words", align_bytes=64)
+
+        def load_x(i, first, count):
+            t0 = i * GROUP + first
+            nc.sync.dma_start(out=x_sb[i][:, first : first + count, :], in_=x_view[:, t0 : t0 + count, :])
+
+        def load_scales(queue, view, side, half):
+            for quad in range(4):
+                first = 32 * quad + 8 * side
+                queue.dma_start(
+                    out=w_planes[first : first + 8, half * FEAT : (half + 1) * FEAT].bitcast(view),
+                    in_=scales_in[side][half][:, 4 * quad : 4 * quad + 4, :].bitcast(view),
+                )
+
+        def load_words(side):
+            for half in range(2):
+                nc.sync.dma_start(
+                    out=w_words[:, :, side, half * FEAT : (half + 1) * FEAT].bitcast(I32),
+                    in_=words_in[side][half].rearrange("g p n t -> p g (n t)").bitcast(I32),
+                )
+
+        load_x(0, 0, 2)
+        load_x(0, 2, 2)
+        load_x(1, 0, GROUP)
+        load_scales(nc.sync, I32, 0, 0)
+        load_scales(nc.gpsimd, F32, 1, 0)
+        load_scales(nc.gpsimd, F32, 1, 1)
+        load_x(2, 0, GROUP)
+        load_words(1)
+        load_scales(nc.sync, I32, 0, 1)
+        load_words(0)
+        for i in range(3, GROUPS):
+            load_x(i, 0, GROUP)
+
+        codes = {}
+        planes = {}
+        blended = {}
+
+        def prepare(i):
+            for j in range(GROUP):
+                t = i * GROUP + j
+                words = x_sb[i][:, j, :].bitcast(F32)
+                xt = psum_t.tile([P, PASSES, 2, P], F32, name="xt")
+                for g in range(PASSES):
+                    for u in range(2):
+                        nc.tensor.transpose(
+                            xt[:, g, u, :], words[:, g * 256 + u : (g + 1) * 256 : 2], ident[:]
+                        )
+                grouped = stage.tile([P, PASSES * P * 4], BF16, name="grouped", align_bytes=64)
+                nc.scalar.copy(
+                    out=grouped[:].bitcast(F32).rearrange("p (g r u) -> p g r u", g=PASSES, u=2),
+                    in_=xt[:].rearrange("p g u r -> p g r u"),
+                )
+                codes[t] = ahead.tile([P, PASSES * P], U32, name="codes", align_bytes=64)
+                planes[t] = ahead.tile([P, PASSES * P], U8, name="planes", align_bytes=64)
+                nc.vector.quantize_mx(out=codes[t][:].bitcast(FP8X4), scales=planes[t][:], in_=grouped[:])
+
+        def blend_biases_on_vector(i):
+            for t in range(i * GROUP, (i + 1) * GROUP):
+                blended[t] = ahead.tile([P, BANK], F32, name="blended")
+                nc.vector.scalar_tensor_tensor(
+                    out=blended[t][:], in0=bias_diff[:], scalar=m_f[:, t : t + 1], in1=bias_base[:],
+                    op0=MULT, op1=ADD,
+                )
+
+        def blend_biases(i):
+            for t in range(i * GROUP, (i + 1) * GROUP):
+                blended[t] = ahead.tile([P, BANK], F32, name="blended")
+                nc.scalar.activation(out=blended[t][:], in_=bias_diff[:], func=COPY, scale=m_f[:, t : t + 1])
+                nc.gpsimd.tensor_tensor(out=blended[t][:], in0=blended[t][:], in1=bias_base[:], op=ADD)
+
+        def project(i):
+            for t in range(i * GROUP, (i + 1) * GROUP):
+                acc = [
+                    psum_mm.tile([P, BANK], F32, name="acc_base"),
+                    psum_mm.tile([P, BANK], F32, name="acc_reas"),
+                ]
+                for side in (1, 0):
+                    for g in range(PASSES):
+                        first = 8 * side + 4 * g
+                        nc.tensor.matmul_mx(
+                            out=acc[side][:],
+                            lhsT=codes[t][:, g * P : (g + 1) * P].bitcast(FP8X4),
+                            lhsT_scale=planes[t][:, g * P : (g + 1) * P],
+                            rhs=w_words[:, g, side, :].bitcast(FP8X4),
+                            rhs_scale=w_planes[first:P, :],
+                            start=(g == 0),
+                            stop=(g == PASSES - 1),
+                        )
+                part = stage.tile([P, BANK], F32, name="part")
+                nc.vector.scalar_tensor_tensor(
+                    out=part[:], in0=acc[1][:], scalar=m_f[:, t : t + 1], in1=blended[t][:], op0=MULT, op1=ADD
+                )
+                result = stage.tile([P, BANK], F32, name="result")
+                nc.vector.scalar_tensor_tensor(
+                    out=result[:], in0=acc[0][:], scalar=one_minus_m[:, t : t + 1], in1=part[:], op0=MULT, op1=ADD
+                )
+                for half in range(2):
+                    nc.sync.dma_start(out=out_views[half][:, t, :], in_=result[:, half * FEAT : (half + 1) * FEAT])
+
+        prepare(0)
+
+        m_f = keep.tile([P, TILES], F32, name="m_f")
+        nc.vector.tensor_copy(out=m_f[:], in_=m_bf[:])
+        one_minus_m = keep.tile([P, TILES], F32, name="one_minus_m")
+        nc.vector.tensor_scalar(out=one_minus_m[:], in0=m_f[:], scalar1=-1.0, scalar2=1.0, op0=MULT, op1=ADD)
+        base_ps = psum_mm.tile([P, BANK], F32, name="base_ps", tag="acc_base")
+        nc.tensor.matmul(out=base_ps[:], lhsT=ones[:], rhs=bias_rows[:, 0, :], start=True, stop=True)
+        reas_ps = psum_mm.tile([P, BANK], F32, name="reas_ps", tag="acc_reas")
+        nc.tensor.matmul(out=reas_ps[:], lhsT=ones[:], rhs=bias_rows[:, 1, :], start=True, stop=True)
+        bias_base = keep.tile([P, BANK], F32, name="bias_base")
+        nc.vector.tensor_copy(out=bias_base[:], in_=base_ps[:])
+        bias_diff = keep.tile([P, BANK], F32, name="bias_diff")
+        nc.vector.tensor_tensor(out=bias_diff[:], in0=reas_ps[:], in1=bias_base[:], op=SUBTRACT)
+
+        blend_biases_on_vector(0)
+        for i in range(1, LOOKAHEAD):
+            prepare(i)
+        for i in range(GROUPS):
+            if i + LOOKAHEAD < GROUPS:
+                prepare(i + LOOKAHEAD)
+            if i + 1 < GROUPS:
+                blend_biases(i + 1)
+            project(i)

@@ -11,8 +11,6 @@ U8 = mybir.dt.uint8
 FP8X4 = mybir.dt.float8_e4m3fn_x4
 MULT = mybir.AluOpType.mult
 ADD = mybir.AluOpType.add
-SUBTRACT = mybir.AluOpType.subtract
-COPY = mybir.ActivationFunctionType.Copy
 
 P = 128
 TOKENS = 4096
@@ -24,7 +22,6 @@ BANK = 2 * FEAT
 TILES = TOKENS // P
 GROUP = 4
 GROUPS = TILES // GROUP
-LOOKAHEAD = 3
 
 FLOPS = 2 * TOKENS * HID * 4 * FEAT
 
@@ -36,10 +33,10 @@ def tile_reasoningmultiheadattention_pa_t_kernel(
     out_0, out_1,
 ):
     nc = tc.nc
-    x_view = x.rearrange("b s k -> (b s) k").rearrange("(p t) k -> p t k", t=TILES)
-    m_view = reasoning_mask.rearrange("b s o i -> (b s o i)").rearrange("(p t) -> p t", t=TILES)
+    x_view = x.rearrange("b s k -> (b s) k").rearrange("(t p) k -> p t k", p=P)
+    gate_flat = reasoning_mask.rearrange("b s o i -> (b s o i)")
     out_views = [
-        o.rearrange("b s h d -> (b s) (h d)").rearrange("(p t) n -> p t n", t=TILES) for o in (out_0, out_1)
+        o.rearrange("b s h d -> (b s) (h d)").rearrange("(t p) n -> p t n", p=P) for o in (out_0, out_1)
     ]
     words_in = [[Wq_words, Wk_words], [Wqr_words, Wkr_words]]
     scales_in = [[Wq_scales, Wk_scales], [Wqr_scales, Wkr_scales]]
@@ -49,26 +46,27 @@ def tile_reasoningmultiheadattention_pa_t_kernel(
         ctx.enter_context(tc.manual_schedule())
         keep = ctx.enter_context(tc.tile_pool(name="keep", bufs=1))
         stage = ctx.enter_context(tc.tile_pool(name="stage", bufs=6))
-        ahead = ctx.enter_context(tc.tile_pool(name="ahead", bufs=(LOOKAHEAD + 1) * GROUP))
-        psum_t = ctx.enter_context(tc.psum_pool(name="psum_t", bufs=4))
+        psum_t = ctx.enter_context(tc.psum_pool(name="psum_t", bufs=3))
         psum_mm = ctx.enter_context(tc.psum_pool(name="psum_mm", bufs=2))
 
         ident = keep.tile([P, P], F32, name="ident")
         make_identity(nc, ident[:])
-        ones = keep.tile([P, P], BF16, name="ones")
-        nc.vector.memset(ones[:], 1.0)
-        bias_rows = keep.tile([P, 2, BANK], BF16, name="bias_rows")
+        bias_rows = keep.tile([P, BANK], BF16, name="bias_rows")
         nc.vector.memset(bias_rows[:], 0.0)
         w_planes = keep.tile([P, BANK], U8, name="w_planes", align_bytes=64)
         nc.vector.memset(w_planes[:].bitcast(I32), 0)
-        for side in range(2):
-            for half in range(2):
-                nc.scalar.dma_start(
-                    out=bias_rows[0:1, side, half * FEAT : (half + 1) * FEAT],
-                    in_=bias_in[side][half].unsqueeze(0),
-                )
-        m_bf = keep.tile([P, TILES], BF16, name="m_bf")
-        nc.scalar.dma_start(out=m_bf[:], in_=m_view)
+        gate_by_tile = keep.tile([P, P], F32, name="gate_by_tile")
+        nc.vector.memset(gate_by_tile[:], 0.0)
+        gate_rows = keep.tile([P, TOKENS], BF16, name="gate_rows")
+        nc.vector.memset(gate_rows[:].bitcast(I32), 0)
+        nc.vector.memset(gate_rows[0:32, :], 1.0)
+        for half in range(2):
+            cols = slice(half * FEAT, (half + 1) * FEAT)
+            nc.scalar.dma_start(out=bias_rows[0:P:64, cols], in_=bias_in[0][half].unsqueeze(0).to_broadcast([2, FEAT]))
+            nc.scalar.dma_start(out=bias_rows[32:33, cols], in_=bias_in[1][half].unsqueeze(0))
+        nc.scalar.dma_start(out=gate_rows[32:65:32, :], in_=gate_flat.unsqueeze(0).to_broadcast([2, TOKENS]))
+        gate_by_tile_bf = keep.tile([TILES, P], BF16, name="gate_by_tile_bf")
+        nc.scalar.dma_start(out=gate_by_tile_bf[:], in_=gate_flat.rearrange("(t p) -> t p", p=P))
 
         x_sb = [keep.tile([P, GROUP, HID], BF16, name="x%d" % i) for i in range(GROUPS)]
         w_words = keep.tile([P, PASSES, 2, BANK], U32, name="w_words", align_bytes=64)
@@ -77,13 +75,12 @@ def tile_reasoningmultiheadattention_pa_t_kernel(
             t0 = i * GROUP + first
             nc.sync.dma_start(out=x_sb[i][:, first : first + count, :], in_=x_view[:, t0 : t0 + count, :])
 
-        def load_scales(queue, view, side, half):
-            for quad in range(4):
-                first = 32 * quad + 8 * side
-                queue.dma_start(
-                    out=w_planes[first : first + 8, half * FEAT : (half + 1) * FEAT].bitcast(view),
-                    in_=scales_in[side][half][:, 4 * quad : 4 * quad + 4, :].bitcast(view),
-                )
+        def load_scale_rows(side, half, quad):
+            first = 32 * quad + 8 * side
+            nc.sync.dma_start(
+                out=w_planes[first : first + 8, half * FEAT : (half + 1) * FEAT].bitcast(I32),
+                in_=scales_in[side][half][:, 4 * quad : 4 * quad + 4, :].bitcast(I32),
+            )
 
         def load_words(side):
             for half in range(2):
@@ -92,21 +89,20 @@ def tile_reasoningmultiheadattention_pa_t_kernel(
                     in_=words_in[side][half].rearrange("g p n t -> p g (n t)").bitcast(I32),
                 )
 
-        load_x(0, 0, 2)
-        load_x(0, 2, 2)
-        load_x(1, 0, GROUP)
-        load_scales(nc.sync, I32, 0, 0)
-        load_scales(nc.gpsimd, F32, 1, 0)
-        load_scales(nc.gpsimd, F32, 1, 1)
-        load_x(2, 0, GROUP)
+        scale_pieces = [(side, half, quad) for side in range(2) for half in range(2) for quad in range(4)]
+        for i in range(GROUPS):
+            if i == 0:
+                load_x(0, 0, 2)
+                load_x(0, 2, 2)
+            else:
+                load_x(i, 0, GROUP)
+            for piece in scale_pieces[2 * i : 2 * i + 2]:
+                load_scale_rows(*piece)
         load_words(1)
-        load_scales(nc.sync, I32, 0, 1)
         load_words(0)
-        for i in range(3, GROUPS):
-            load_x(i, 0, GROUP)
 
-        codes = {}
-        planes = {}
+        codes = keep.tile([P, TILES, PASSES * P], U32, name="codes", align_bytes=64)
+        planes = keep.tile([P, TILES, PASSES * P], U8, name="planes", align_bytes=64)
         blended = {}
 
         def prepare(i):
@@ -124,26 +120,20 @@ def tile_reasoningmultiheadattention_pa_t_kernel(
                     out=grouped[:].bitcast(F32).rearrange("p (g r u) -> p g r u", g=PASSES, u=2),
                     in_=xt[:].rearrange("p g u r -> p g r u"),
                 )
-                codes[t] = ahead.tile([P, PASSES * P], U32, name="codes", align_bytes=64)
-                planes[t] = ahead.tile([P, PASSES * P], U8, name="planes", align_bytes=64)
-                nc.vector.quantize_mx(out=codes[t][:].bitcast(FP8X4), scales=planes[t][:], in_=grouped[:])
+                nc.vector.quantize_mx(out=codes[:, t, :].bitcast(FP8X4), scales=planes[:, t, :], in_=grouped[:])
 
-        def blend_biases_on_vector(i):
-            for t in range(i * GROUP, (i + 1) * GROUP):
-                blended[t] = ahead.tile([P, BANK], F32, name="blended")
-                nc.vector.scalar_tensor_tensor(
-                    out=blended[t][:], in0=bias_diff[:], scalar=m_f[:, t : t + 1], in1=bias_base[:],
-                    op0=MULT, op1=ADD,
-                )
-
-        def blend_biases(i):
-            for t in range(i * GROUP, (i + 1) * GROUP):
-                blended[t] = ahead.tile([P, BANK], F32, name="blended")
-                nc.scalar.activation(out=blended[t][:], in_=bias_diff[:], func=COPY, scale=m_f[:, t : t + 1])
-                nc.gpsimd.tensor_tensor(out=blended[t][:], in0=blended[t][:], in1=bias_base[:], op=ADD)
+        def blend_biases(t):
+            blend_ps = psum_mm.tile([P, BANK], F32, name="blend_ps", bufs=1)
+            nc.tensor.matmul(
+                out=blend_ps[:], lhsT=gate_rows[:, t * P : (t + 1) * P], rhs=bias_rows[:], start=True, stop=True
+            )
+            blended[t] = stage.tile([P, BANK], F32, name="blended")
+            nc.scalar.copy(out=blended[t][:], in_=blend_ps[:])
 
         def project(i):
             for t in range(i * GROUP, (i + 1) * GROUP):
+                if t + 1 < TILES:
+                    blend_biases(t + 1)
                 acc = [
                     psum_mm.tile([P, BANK], F32, name="acc_base"),
                     psum_mm.tile([P, BANK], F32, name="acc_reas"),
@@ -153,8 +143,8 @@ def tile_reasoningmultiheadattention_pa_t_kernel(
                         first = 8 * side + 4 * g
                         nc.tensor.matmul_mx(
                             out=acc[side][:],
-                            lhsT=codes[t][:, g * P : (g + 1) * P].bitcast(FP8X4),
-                            lhsT_scale=planes[t][:, g * P : (g + 1) * P],
+                            lhsT=codes[:, t, g * P : (g + 1) * P].bitcast(FP8X4),
+                            lhsT_scale=planes[:, t, g * P : (g + 1) * P],
                             rhs=w_words[:, g, side, :].bitcast(FP8X4),
                             rhs_scale=w_planes[first:P, :],
                             start=(g == 0),
@@ -171,27 +161,21 @@ def tile_reasoningmultiheadattention_pa_t_kernel(
                 for half in range(2):
                     nc.sync.dma_start(out=out_views[half][:, t, :], in_=result[:, half * FEAT : (half + 1) * FEAT])
 
-        prepare(0)
+        for i in range(GROUPS // 2):
+            prepare(i)
 
+        nc.vector.tensor_scalar_mul(out=bias_rows[64:96, :], in0=bias_rows[64:96, :], scalar1=-1.0)
+        nc.vector.tensor_copy(out=gate_by_tile[0:TILES, :], in_=gate_by_tile_bf[:])
+        gate_ps = psum_mm.tile([P, P], F32, name="gate_ps", tag="blend_ps", bufs=1)
+        nc.tensor.transpose(gate_ps[:], gate_by_tile[:], ident[:])
         m_f = keep.tile([P, TILES], F32, name="m_f")
-        nc.vector.tensor_copy(out=m_f[:], in_=m_bf[:])
+        nc.vector.tensor_copy(out=m_f[:], in_=gate_ps[:, 0:TILES])
         one_minus_m = keep.tile([P, TILES], F32, name="one_minus_m")
         nc.vector.tensor_scalar(out=one_minus_m[:], in0=m_f[:], scalar1=-1.0, scalar2=1.0, op0=MULT, op1=ADD)
-        base_ps = psum_mm.tile([P, BANK], F32, name="base_ps", tag="acc_base")
-        nc.tensor.matmul(out=base_ps[:], lhsT=ones[:], rhs=bias_rows[:, 0, :], start=True, stop=True)
-        reas_ps = psum_mm.tile([P, BANK], F32, name="reas_ps", tag="acc_reas")
-        nc.tensor.matmul(out=reas_ps[:], lhsT=ones[:], rhs=bias_rows[:, 1, :], start=True, stop=True)
-        bias_base = keep.tile([P, BANK], F32, name="bias_base")
-        nc.vector.tensor_copy(out=bias_base[:], in_=base_ps[:])
-        bias_diff = keep.tile([P, BANK], F32, name="bias_diff")
-        nc.vector.tensor_tensor(out=bias_diff[:], in0=reas_ps[:], in1=bias_base[:], op=SUBTRACT)
 
-        blend_biases_on_vector(0)
-        for i in range(1, LOOKAHEAD):
+        for i in range(GROUPS // 2, GROUPS):
             prepare(i)
+
+        blend_biases(0)
         for i in range(GROUPS):
-            if i + LOOKAHEAD < GROUPS:
-                prepare(i + LOOKAHEAD)
-            if i + 1 < GROUPS:
-                blend_biases(i + 1)
             project(i)

@@ -11,6 +11,8 @@ U8 = mybir.dt.uint8
 FP8X4 = mybir.dt.float8_e4m3fn_x4
 MULT = mybir.AluOpType.mult
 ADD = mybir.AluOpType.add
+SUBTRACT = mybir.AluOpType.subtract
+COPY = mybir.ActivationFunctionType.Copy
 
 P = 128
 TOKENS = 4096
@@ -22,6 +24,7 @@ BANK = 2 * FEAT
 TILES = TOKENS // P
 GROUP = 4
 GROUPS = TILES // GROUP
+LOOKAHEAD = 2
 
 FLOPS = 2 * TOKENS * HID * 4 * FEAT
 
@@ -33,10 +36,10 @@ def tile_reasoningmultiheadattention_pa_t_kernel(
     out_0, out_1,
 ):
     nc = tc.nc
-    x_view = x.rearrange("b s k -> (b s) k").rearrange("(t p) k -> p t k", p=P)
-    gate_flat = reasoning_mask.rearrange("b s o i -> (b s o i)")
+    x_view = x.rearrange("b s k -> (b s) k").rearrange("(p t) k -> p t k", t=TILES)
+    m_view = reasoning_mask.rearrange("b s o i -> (b s o i)").rearrange("(p t) -> p t", t=TILES)
     out_views = [
-        o.rearrange("b s h d -> (b s) (h d)").rearrange("(t p) n -> p t n", p=P) for o in (out_0, out_1)
+        o.rearrange("b s h d -> (b s) (h d)").rearrange("(p t) n -> p t n", t=TILES) for o in (out_0, out_1)
     ]
     words_in = [[Wq_words, Wk_words], [Wqr_words, Wkr_words]]
     scales_in = [[Wq_scales, Wk_scales], [Wqr_scales, Wkr_scales]]
@@ -46,28 +49,18 @@ def tile_reasoningmultiheadattention_pa_t_kernel(
         ctx.enter_context(tc.manual_schedule())
         keep = ctx.enter_context(tc.tile_pool(name="keep", bufs=1))
         stage = ctx.enter_context(tc.tile_pool(name="stage", bufs=6))
-        psum_t = ctx.enter_context(tc.psum_pool(name="psum_t", bufs=3))
+        ahead = ctx.enter_context(tc.tile_pool(name="ahead", bufs=(LOOKAHEAD + 1) * GROUP))
+        psum_t = ctx.enter_context(tc.psum_pool(name="psum_t", bufs=4))
         psum_mm = ctx.enter_context(tc.psum_pool(name="psum_mm", bufs=2))
 
-        ident = keep.tile([P, P], F32, name="ident")
-        make_identity(nc, ident[:])
-        bias_rows = keep.tile([P, BANK], BF16, name="bias_rows")
-        nc.vector.memset(bias_rows[:], 0.0)
         w_planes = keep.tile([P, BANK], U8, name="w_planes", align_bytes=64)
         nc.vector.memset(w_planes[:].bitcast(I32), 0)
-        gate_by_tile = keep.tile([P, P], F32, name="gate_by_tile")
-        nc.vector.memset(gate_by_tile[:], 0.0)
-        gate_rows = keep.tile([P, TOKENS], BF16, name="gate_rows")
-        nc.vector.memset(gate_rows[:].bitcast(I32), 0)
-        nc.vector.memset(gate_rows[0:32, :], 1.0)
-        for half in range(2):
-            cols = slice(half * FEAT, (half + 1) * FEAT)
-            nc.scalar.dma_start(out=bias_rows[0:P:64, cols], in_=bias_in[0][half].unsqueeze(0).to_broadcast([2, FEAT]))
-            nc.scalar.dma_start(out=bias_rows[32:33, cols], in_=bias_in[1][half].unsqueeze(0))
-        nc.scalar.dma_start(out=gate_rows[32:65:32, :], in_=gate_flat.unsqueeze(0).to_broadcast([2, TOKENS]))
-        gate_by_tile_bf = keep.tile([TILES, P], BF16, name="gate_by_tile_bf")
-        nc.scalar.dma_start(out=gate_by_tile_bf[:], in_=gate_flat.rearrange("(t p) -> t p", p=P))
-
+        ident = keep.tile([P, P], F32, name="ident")
+        make_identity(nc, ident[:])
+        ones = keep.tile([P, P], BF16, name="ones")
+        nc.vector.memset(ones[:], 1.0)
+        bias_rows = keep.tile([P, 2, BANK], BF16, name="bias_rows")
+        nc.vector.memset(bias_rows[:], 0.0)
         x_sb = [keep.tile([P, GROUP, HID], BF16, name="x%d" % i) for i in range(GROUPS)]
         w_words = keep.tile([P, PASSES, 2, BANK], U32, name="w_words", align_bytes=64)
 
@@ -75,12 +68,13 @@ def tile_reasoningmultiheadattention_pa_t_kernel(
             t0 = i * GROUP + first
             nc.sync.dma_start(out=x_sb[i][:, first : first + count, :], in_=x_view[:, t0 : t0 + count, :])
 
-        def load_scale_rows(side, half, quad):
-            first = 32 * quad + 8 * side
-            nc.sync.dma_start(
-                out=w_planes[first : first + 8, half * FEAT : (half + 1) * FEAT].bitcast(I32),
-                in_=scales_in[side][half][:, 4 * quad : 4 * quad + 4, :].bitcast(I32),
-            )
+        def load_scales(side, half):
+            for quad in range(4):
+                first = 32 * quad + 8 * side
+                nc.sync.dma_start(
+                    out=w_planes[first : first + 8, half * FEAT : (half + 1) * FEAT].bitcast(I32),
+                    in_=scales_in[side][half][:, 4 * quad : 4 * quad + 4, :].bitcast(I32),
+                )
 
         def load_words(side):
             for half in range(2):
@@ -89,20 +83,28 @@ def tile_reasoningmultiheadattention_pa_t_kernel(
                     in_=words_in[side][half].rearrange("g p n t -> p g (n t)").bitcast(I32),
                 )
 
-        scale_pieces = [(side, half, quad) for side in range(2) for half in range(2) for quad in range(4)]
-        for i in range(GROUPS):
-            if i == 0:
-                load_x(0, 0, 2)
-                load_x(0, 2, 2)
-            else:
-                load_x(i, 0, GROUP)
-            for piece in scale_pieces[2 * i : 2 * i + 2]:
-                load_scale_rows(*piece)
+        for side in (1, 0):
+            for half in range(2):
+                load_scales(side, half)
+        for side in range(2):
+            for half in range(2):
+                nc.scalar.dma_start(
+                    out=bias_rows[0:1, side, half * FEAT : (half + 1) * FEAT],
+                    in_=bias_in[side][half].unsqueeze(0),
+                )
+        m_bf = keep.tile([P, TILES], BF16, name="m_bf")
+        nc.scalar.dma_start(out=m_bf[:], in_=m_view)
+        load_x(0, 0, 2)
+        load_x(0, 2, 2)
+        load_x(1, 0, GROUP)
+        load_x(2, 0, GROUP)
         load_words(1)
         load_words(0)
+        for i in range(3, GROUPS):
+            load_x(i, 0, GROUP)
 
-        codes = keep.tile([P, TILES, PASSES * P], U32, name="codes", align_bytes=64)
-        planes = keep.tile([P, TILES, PASSES * P], U8, name="planes", align_bytes=64)
+        codes = {}
+        planes = {}
         blended = {}
 
         def prepare(i):
@@ -120,20 +122,26 @@ def tile_reasoningmultiheadattention_pa_t_kernel(
                     out=grouped[:].bitcast(F32).rearrange("p (g r u) -> p g r u", g=PASSES, u=2),
                     in_=xt[:].rearrange("p g u r -> p g r u"),
                 )
-                nc.vector.quantize_mx(out=codes[:, t, :].bitcast(FP8X4), scales=planes[:, t, :], in_=grouped[:])
+                codes[t] = ahead.tile([P, PASSES * P], U32, name="codes", align_bytes=64)
+                planes[t] = ahead.tile([P, PASSES * P], U8, name="planes", align_bytes=64)
+                nc.vector.quantize_mx(out=codes[t][:].bitcast(FP8X4), scales=planes[t][:], in_=grouped[:])
 
-        def blend_biases(t):
-            blend_ps = psum_mm.tile([P, BANK], F32, name="blend_ps", bufs=1)
-            nc.tensor.matmul(
-                out=blend_ps[:], lhsT=gate_rows[:, t * P : (t + 1) * P], rhs=bias_rows[:], start=True, stop=True
-            )
-            blended[t] = stage.tile([P, BANK], F32, name="blended")
-            nc.scalar.copy(out=blended[t][:], in_=blend_ps[:])
+        def blend_biases_on_vector(i):
+            for t in range(i * GROUP, (i + 1) * GROUP):
+                blended[t] = ahead.tile([P, BANK], F32, name="blended")
+                nc.vector.scalar_tensor_tensor(
+                    out=blended[t][:], in0=bias_diff[:], scalar=m_f[:, t : t + 1], in1=bias_base[:],
+                    op0=MULT, op1=ADD,
+                )
+
+        def blend_biases(i):
+            for t in range(i * GROUP, (i + 1) * GROUP):
+                blended[t] = ahead.tile([P, BANK], F32, name="blended")
+                nc.scalar.activation(out=blended[t][:], in_=bias_diff[:], func=COPY, scale=m_f[:, t : t + 1])
+                nc.gpsimd.tensor_tensor(out=blended[t][:], in0=blended[t][:], in1=bias_base[:], op=ADD)
 
         def project(i):
             for t in range(i * GROUP, (i + 1) * GROUP):
-                if t + 1 < TILES:
-                    blend_biases(t + 1)
                 acc = [
                     psum_mm.tile([P, BANK], F32, name="acc_base"),
                     psum_mm.tile([P, BANK], F32, name="acc_reas"),
@@ -143,8 +151,8 @@ def tile_reasoningmultiheadattention_pa_t_kernel(
                         first = 8 * side + 4 * g
                         nc.tensor.matmul_mx(
                             out=acc[side][:],
-                            lhsT=codes[:, t, g * P : (g + 1) * P].bitcast(FP8X4),
-                            lhsT_scale=planes[:, t, g * P : (g + 1) * P],
+                            lhsT=codes[t][:, g * P : (g + 1) * P].bitcast(FP8X4),
+                            lhsT_scale=planes[t][:, g * P : (g + 1) * P],
                             rhs=w_words[:, g, side, :].bitcast(FP8X4),
                             rhs_scale=w_planes[first:P, :],
                             start=(g == 0),
@@ -161,21 +169,27 @@ def tile_reasoningmultiheadattention_pa_t_kernel(
                 for half in range(2):
                     nc.sync.dma_start(out=out_views[half][:, t, :], in_=result[:, half * FEAT : (half + 1) * FEAT])
 
-        for i in range(GROUPS // 2):
-            prepare(i)
+        prepare(0)
 
-        nc.vector.tensor_scalar_mul(out=bias_rows[64:96, :], in0=bias_rows[64:96, :], scalar1=-1.0)
-        nc.vector.tensor_copy(out=gate_by_tile[0:TILES, :], in_=gate_by_tile_bf[:])
-        gate_ps = psum_mm.tile([P, P], F32, name="gate_ps", tag="blend_ps", bufs=1)
-        nc.tensor.transpose(gate_ps[:], gate_by_tile[:], ident[:])
         m_f = keep.tile([P, TILES], F32, name="m_f")
-        nc.vector.tensor_copy(out=m_f[:], in_=gate_ps[:, 0:TILES])
+        nc.vector.tensor_copy(out=m_f[:], in_=m_bf[:])
         one_minus_m = keep.tile([P, TILES], F32, name="one_minus_m")
         nc.vector.tensor_scalar(out=one_minus_m[:], in0=m_f[:], scalar1=-1.0, scalar2=1.0, op0=MULT, op1=ADD)
+        base_ps = psum_mm.tile([P, BANK], F32, name="base_ps", tag="acc_base")
+        nc.tensor.matmul(out=base_ps[:], lhsT=ones[:], rhs=bias_rows[:, 0, :], start=True, stop=True)
+        reas_ps = psum_mm.tile([P, BANK], F32, name="reas_ps", tag="acc_reas")
+        nc.tensor.matmul(out=reas_ps[:], lhsT=ones[:], rhs=bias_rows[:, 1, :], start=True, stop=True)
+        bias_base = keep.tile([P, BANK], F32, name="bias_base")
+        nc.vector.tensor_copy(out=bias_base[:], in_=base_ps[:])
+        bias_diff = keep.tile([P, BANK], F32, name="bias_diff")
+        nc.vector.tensor_tensor(out=bias_diff[:], in0=reas_ps[:], in1=bias_base[:], op=SUBTRACT)
 
-        for i in range(GROUPS // 2, GROUPS):
+        blend_biases_on_vector(0)
+        for i in range(1, LOOKAHEAD):
             prepare(i)
-
-        blend_biases(0)
         for i in range(GROUPS):
+            if i + LOOKAHEAD < GROUPS:
+                prepare(i + LOOKAHEAD)
+            if i + 1 < GROUPS:
+                blend_biases(i + 1)
             project(i)

@@ -11,8 +11,6 @@ U8 = mybir.dt.uint8
 FP8X4 = mybir.dt.float8_e4m3fn_x4
 MULT = mybir.AluOpType.mult
 ADD = mybir.AluOpType.add
-SUBTRACT = mybir.AluOpType.subtract
-COPY = mybir.ActivationFunctionType.Copy
 
 P = 128
 TOKENS = 4096
@@ -24,7 +22,7 @@ BANK = 2 * FEAT
 TILES = TOKENS // P
 GROUP = 4
 GROUPS = TILES // GROUP
-LOOKAHEAD = 2
+BLENDS_AHEAD = 16
 
 FLOPS = 2 * TOKENS * HID * 4 * FEAT
 
@@ -36,10 +34,10 @@ def tile_reasoningmultiheadattention_pa_t_kernel(
     out_0, out_1,
 ):
     nc = tc.nc
-    x_view = x.rearrange("b s k -> (b s) k").rearrange("(p t) k -> p t k", t=TILES)
-    m_view = reasoning_mask.rearrange("b s o i -> (b s o i)").rearrange("(p t) -> p t", t=TILES)
+    x_view = x.rearrange("b s k -> (b s) k").rearrange("(t p) k -> p t k", p=P)
+    gate_flat = reasoning_mask.rearrange("b s o i -> (b s o i)")
     out_views = [
-        o.rearrange("b s h d -> (b s) (h d)").rearrange("(p t) n -> p t n", t=TILES) for o in (out_0, out_1)
+        o.rearrange("b s h d -> (b s) (h d)").rearrange("(t p) n -> p t n", p=P) for o in (out_0, out_1)
     ]
     words_in = [[Wq_words, Wk_words], [Wqr_words, Wkr_words]]
     scales_in = [[Wq_scales, Wk_scales], [Wqr_scales, Wkr_scales]]
@@ -49,18 +47,38 @@ def tile_reasoningmultiheadattention_pa_t_kernel(
         ctx.enter_context(tc.manual_schedule())
         keep = ctx.enter_context(tc.tile_pool(name="keep", bufs=1))
         stage = ctx.enter_context(tc.tile_pool(name="stage", bufs=6))
-        ahead = ctx.enter_context(tc.tile_pool(name="ahead", bufs=(LOOKAHEAD + 1) * GROUP))
+        ahead = ctx.enter_context(tc.tile_pool(name="ahead", bufs=2 * GROUP))
+        biases = ctx.enter_context(tc.tile_pool(name="biases", bufs=BLENDS_AHEAD + 2))
         psum_t = ctx.enter_context(tc.psum_pool(name="psum_t", bufs=4))
         psum_mm = ctx.enter_context(tc.psum_pool(name="psum_mm", bufs=2))
 
-        w_planes = keep.tile([P, BANK], U8, name="w_planes", align_bytes=64)
-        nc.vector.memset(w_planes[:].bitcast(I32), 0)
         ident = keep.tile([P, P], F32, name="ident")
         make_identity(nc, ident[:])
-        ones = keep.tile([P, P], BF16, name="ones")
-        nc.vector.memset(ones[:], 1.0)
-        bias_rows = keep.tile([P, 2, BANK], BF16, name="bias_rows")
+        w_planes = keep.tile([P, BANK], U8, name="w_planes", align_bytes=64)
+        nc.vector.memset(w_planes[:].bitcast(I32), 0)
+        bias_rows = keep.tile([P, BANK], BF16, name="bias_rows")
         nc.vector.memset(bias_rows[:], 0.0)
+        gate_by_tile = keep.tile([P, P], F32, name="gate_by_tile")
+        nc.vector.memset(gate_by_tile[:], 0.0)
+        gate_rows = [keep.tile([P, TOKENS // 2], BF16, name="gate_rows%d" % h) for h in range(2)]
+        gate_by_tile_bf = keep.tile([TILES, P], BF16, name="gate_by_tile_bf")
+        nc.scalar.dma_start(out=gate_by_tile_bf[:], in_=gate_flat.rearrange("(t p) -> t p", p=P))
+        for half in range(2):
+            cols = slice(half * FEAT, (half + 1) * FEAT)
+            nc.scalar.dma_start(out=bias_rows[0:P:64, cols], in_=bias_in[0][half].unsqueeze(0).to_broadcast([2, FEAT]))
+            nc.scalar.dma_start(out=bias_rows[32:33, cols], in_=bias_in[1][half].unsqueeze(0))
+        for h in range(2):
+            nc.vector.memset(gate_rows[h][:].bitcast(I32), 0)
+            nc.vector.memset(gate_rows[h][0:32, :], 1.0)
+
+        def load_gate_rows(queue, h):
+            tokens = slice(h * (TOKENS // 2), (h + 1) * (TOKENS // 2))
+            queue.dma_start(
+                out=gate_rows[h][32:65:32, :], in_=gate_flat[tokens].unsqueeze(0).to_broadcast([2, TOKENS // 2])
+            )
+
+        load_gate_rows(nc.scalar, 0)
+
         x_sb = [keep.tile([P, GROUP, HID], BF16, name="x%d" % i) for i in range(GROUPS)]
         w_words = keep.tile([P, PASSES, 2, BANK], U32, name="w_words", align_bytes=64)
 
@@ -68,8 +86,8 @@ def tile_reasoningmultiheadattention_pa_t_kernel(
             t0 = i * GROUP + first
             nc.sync.dma_start(out=x_sb[i][:, first : first + count, :], in_=x_view[:, t0 : t0 + count, :])
 
-        def load_scales(side, half):
-            for quad in range(4):
+        def load_scale_rows(pieces):
+            for side, half, quad in pieces:
                 first = 32 * quad + 8 * side
                 nc.sync.dma_start(
                     out=w_planes[first : first + 8, half * FEAT : (half + 1) * FEAT].bitcast(I32),
@@ -83,65 +101,67 @@ def tile_reasoningmultiheadattention_pa_t_kernel(
                     in_=words_in[side][half].rearrange("g p n t -> p g (n t)").bitcast(I32),
                 )
 
-        for side in (1, 0):
-            for half in range(2):
-                load_scales(side, half)
-        for side in range(2):
-            for half in range(2):
-                nc.scalar.dma_start(
-                    out=bias_rows[0:1, side, half * FEAT : (half + 1) * FEAT],
-                    in_=bias_in[side][half].unsqueeze(0),
-                )
-        m_bf = keep.tile([P, TILES], BF16, name="m_bf")
-        nc.scalar.dma_start(out=m_bf[:], in_=m_view)
+        scale_pieces = [(side, half, quad) for side in (1, 0) for half in range(2) for quad in range(4)]
         load_x(0, 0, 2)
+        load_scale_rows(scale_pieces[0:2])
         load_x(0, 2, 2)
+        load_scale_rows(scale_pieces[2:4])
         load_x(1, 0, GROUP)
-        load_x(2, 0, GROUP)
+        load_scale_rows(scale_pieces[4:8])
         load_words(1)
+        load_scale_rows(scale_pieces[8:12])
         load_words(0)
-        for i in range(3, GROUPS):
+        load_scale_rows(scale_pieces[12:16])
+        load_gate_rows(nc.sync, 1)
+        for i in range(2, GROUPS):
             load_x(i, 0, GROUP)
 
         codes = {}
         planes = {}
         blended = {}
 
-        def prepare(i):
+        grouped = {}
+
+        def transpose_group(i):
             for j in range(GROUP):
                 t = i * GROUP + j
                 words = x_sb[i][:, j, :].bitcast(F32)
-                xt = psum_t.tile([P, PASSES, 2, P], F32, name="xt")
+                xt = psum_t.tile([P, PASSES, 2, P], F32, name="xt", tag="bank")
                 for g in range(PASSES):
                     for u in range(2):
                         nc.tensor.transpose(
                             xt[:, g, u, :], words[:, g * 256 + u : (g + 1) * 256 : 2], ident[:]
                         )
-                grouped = stage.tile([P, PASSES * P * 4], BF16, name="grouped", align_bytes=64)
+                grouped[t] = ahead.tile([P, PASSES * P * 4], BF16, name="grouped", align_bytes=64)
                 nc.scalar.copy(
-                    out=grouped[:].bitcast(F32).rearrange("p (g r u) -> p g r u", g=PASSES, u=2),
+                    out=grouped[t][:].bitcast(F32).rearrange("p (g r u) -> p g r u", g=PASSES, u=2),
                     in_=xt[:].rearrange("p g u r -> p g r u"),
                 )
-                codes[t] = ahead.tile([P, PASSES * P], U32, name="codes", align_bytes=64)
-                planes[t] = ahead.tile([P, PASSES * P], U8, name="planes", align_bytes=64)
-                nc.vector.quantize_mx(out=codes[t][:].bitcast(FP8X4), scales=planes[t][:], in_=grouped[:])
 
-        def blend_biases_on_vector(i):
-            for t in range(i * GROUP, (i + 1) * GROUP):
-                blended[t] = ahead.tile([P, BANK], F32, name="blended")
-                nc.vector.scalar_tensor_tensor(
-                    out=blended[t][:], in0=bias_diff[:], scalar=m_f[:, t : t + 1], in1=bias_base[:],
-                    op0=MULT, op1=ADD,
-                )
+        def quantise(t):
+            codes[t] = ahead.tile([P, PASSES * P], U32, name="codes", align_bytes=64)
+            planes[t] = ahead.tile([P, PASSES * P], U8, name="planes", align_bytes=64)
+            nc.vector.quantize_mx(out=codes[t][:].bitcast(FP8X4), scales=planes[t][:], in_=grouped[t][:])
 
-        def blend_biases(i):
-            for t in range(i * GROUP, (i + 1) * GROUP):
-                blended[t] = ahead.tile([P, BANK], F32, name="blended")
-                nc.scalar.activation(out=blended[t][:], in_=bias_diff[:], func=COPY, scale=m_f[:, t : t + 1])
-                nc.gpsimd.tensor_tensor(out=blended[t][:], in0=blended[t][:], in1=bias_base[:], op=ADD)
+        def blend_biases(t):
+            blend_ps = psum_t.tile([P, BANK], F32, name="blend_ps", tag="bank")
+            nc.tensor.matmul(
+                out=blend_ps[:],
+                lhsT=gate_rows[t // (TILES // 2)][:, (t % (TILES // 2)) * P : (t % (TILES // 2) + 1) * P],
+                rhs=bias_rows[:],
+                start=True,
+                stop=True,
+            )
+            blended[t] = biases.tile([P, BANK], F32, name="blended")
+            if t < BLENDS_AHEAD and t % 2 == 1:
+                nc.vector.tensor_copy(out=blended[t][:], in_=blend_ps[:])
+            else:
+                nc.scalar.copy(out=blended[t][:], in_=blend_ps[:])
 
         def project(i):
             for t in range(i * GROUP, (i + 1) * GROUP):
+                if t + BLENDS_AHEAD < TILES:
+                    blend_biases(t + BLENDS_AHEAD)
                 acc = [
                     psum_mm.tile([P, BANK], F32, name="acc_base"),
                     psum_mm.tile([P, BANK], F32, name="acc_reas"),
@@ -162,6 +182,8 @@ def tile_reasoningmultiheadattention_pa_t_kernel(
                 nc.vector.scalar_tensor_tensor(
                     out=part[:], in0=acc[1][:], scalar=m_f[:, t : t + 1], in1=blended[t][:], op0=MULT, op1=ADD
                 )
+                if t + GROUP < TILES:
+                    quantise(t + GROUP)
                 result = stage.tile([P, BANK], F32, name="result")
                 nc.vector.scalar_tensor_tensor(
                     out=result[:], in0=acc[0][:], scalar=one_minus_m[:, t : t + 1], in1=part[:], op0=MULT, op1=ADD
@@ -169,27 +191,22 @@ def tile_reasoningmultiheadattention_pa_t_kernel(
                 for half in range(2):
                     nc.sync.dma_start(out=out_views[half][:, t, :], in_=result[:, half * FEAT : (half + 1) * FEAT])
 
-        prepare(0)
+        transpose_group(0)
+        for t in range(GROUP):
+            quantise(t)
 
+        nc.vector.tensor_scalar_mul(out=bias_rows[64:96, :], in0=bias_rows[64:96, :], scalar1=-1.0)
+        nc.vector.tensor_copy(out=gate_by_tile[0:TILES, :], in_=gate_by_tile_bf[:])
+        gate_ps = psum_t.tile([P, P], F32, name="gate_ps", tag="bank")
+        nc.tensor.transpose(gate_ps[:], gate_by_tile[:], ident[:])
         m_f = keep.tile([P, TILES], F32, name="m_f")
-        nc.vector.tensor_copy(out=m_f[:], in_=m_bf[:])
+        nc.vector.tensor_copy(out=m_f[:], in_=gate_ps[:, 0:TILES])
         one_minus_m = keep.tile([P, TILES], F32, name="one_minus_m")
         nc.vector.tensor_scalar(out=one_minus_m[:], in0=m_f[:], scalar1=-1.0, scalar2=1.0, op0=MULT, op1=ADD)
-        base_ps = psum_mm.tile([P, BANK], F32, name="base_ps", tag="acc_base")
-        nc.tensor.matmul(out=base_ps[:], lhsT=ones[:], rhs=bias_rows[:, 0, :], start=True, stop=True)
-        reas_ps = psum_mm.tile([P, BANK], F32, name="reas_ps", tag="acc_reas")
-        nc.tensor.matmul(out=reas_ps[:], lhsT=ones[:], rhs=bias_rows[:, 1, :], start=True, stop=True)
-        bias_base = keep.tile([P, BANK], F32, name="bias_base")
-        nc.vector.tensor_copy(out=bias_base[:], in_=base_ps[:])
-        bias_diff = keep.tile([P, BANK], F32, name="bias_diff")
-        nc.vector.tensor_tensor(out=bias_diff[:], in0=reas_ps[:], in1=bias_base[:], op=SUBTRACT)
 
-        blend_biases_on_vector(0)
-        for i in range(1, LOOKAHEAD):
-            prepare(i)
+        for t in range(BLENDS_AHEAD):
+            blend_biases(t)
         for i in range(GROUPS):
-            if i + LOOKAHEAD < GROUPS:
-                prepare(i + LOOKAHEAD)
             if i + 1 < GROUPS:
-                blend_biases(i + 1)
+                transpose_group(i + 1)
             project(i)

@@ -11,6 +11,8 @@ U8 = mybir.dt.uint8
 FP8X4 = mybir.dt.float8_e4m3fn_x4
 MULT = mybir.AluOpType.mult
 ADD = mybir.AluOpType.add
+SUBTRACT = mybir.AluOpType.subtract
+COPY = mybir.ActivationFunctionType.Copy
 
 P = 128
 TOKENS = 4096
@@ -22,7 +24,7 @@ BANK = 2 * FEAT
 TILES = TOKENS // P
 GROUP = 4
 GROUPS = TILES // GROUP
-BLENDS_AHEAD = 16
+LOOKAHEAD = 1
 
 FLOPS = 2 * TOKENS * HID * 4 * FEAT
 
@@ -34,10 +36,10 @@ def tile_reasoningmultiheadattention_pa_t_kernel(
     out_0, out_1,
 ):
     nc = tc.nc
-    x_view = x.rearrange("b s k -> (b s) k").rearrange("(t p) k -> p t k", p=P)
-    gate_flat = reasoning_mask.rearrange("b s o i -> (b s o i)")
+    x_view = x.rearrange("b s k -> (b s) k").rearrange("(p t) k -> p t k", t=TILES)
+    m_view = reasoning_mask.rearrange("b s o i -> (b s o i)").rearrange("(p t) -> p t", t=TILES)
     out_views = [
-        o.rearrange("b s h d -> (b s) (h d)").rearrange("(t p) n -> p t n", p=P) for o in (out_0, out_1)
+        o.rearrange("b s h d -> (b s) (h d)").rearrange("(p t) n -> p t n", t=TILES) for o in (out_0, out_1)
     ]
     words_in = [[Wq_words, Wk_words], [Wqr_words, Wkr_words]]
     scales_in = [[Wq_scales, Wk_scales], [Wqr_scales, Wkr_scales]]
@@ -47,38 +49,17 @@ def tile_reasoningmultiheadattention_pa_t_kernel(
         ctx.enter_context(tc.manual_schedule())
         keep = ctx.enter_context(tc.tile_pool(name="keep", bufs=1))
         stage = ctx.enter_context(tc.tile_pool(name="stage", bufs=6))
-        ahead = ctx.enter_context(tc.tile_pool(name="ahead", bufs=2 * GROUP))
-        biases = ctx.enter_context(tc.tile_pool(name="biases", bufs=BLENDS_AHEAD + 2))
-        psum_t = ctx.enter_context(tc.psum_pool(name="psum_t", bufs=4))
-        psum_mm = ctx.enter_context(tc.psum_pool(name="psum_mm", bufs=2))
+        ahead = ctx.enter_context(tc.tile_pool(name="ahead", bufs=(LOOKAHEAD + 1) * GROUP))
+        psum = ctx.enter_context(tc.psum_pool(name="psum", bufs=8))
 
-        ident = keep.tile([P, P], F32, name="ident")
-        make_identity(nc, ident[:])
         w_planes = keep.tile([P, BANK], U8, name="w_planes", align_bytes=64)
         nc.vector.memset(w_planes[:].bitcast(I32), 0)
-        bias_rows = keep.tile([P, BANK], BF16, name="bias_rows")
+        ident = keep.tile([P, P], F32, name="ident")
+        make_identity(nc, ident[:])
+        ones = keep.tile([P, P], BF16, name="ones")
+        nc.vector.memset(ones[:], 1.0)
+        bias_rows = keep.tile([P, 2, BANK], BF16, name="bias_rows")
         nc.vector.memset(bias_rows[:], 0.0)
-        gate_by_tile = keep.tile([P, P], F32, name="gate_by_tile")
-        nc.vector.memset(gate_by_tile[:], 0.0)
-        gate_rows = [keep.tile([P, TOKENS // 2], BF16, name="gate_rows%d" % h) for h in range(2)]
-        gate_by_tile_bf = keep.tile([TILES, P], BF16, name="gate_by_tile_bf")
-        nc.scalar.dma_start(out=gate_by_tile_bf[:], in_=gate_flat.rearrange("(t p) -> t p", p=P))
-        for half in range(2):
-            cols = slice(half * FEAT, (half + 1) * FEAT)
-            nc.scalar.dma_start(out=bias_rows[0:P:64, cols], in_=bias_in[0][half].unsqueeze(0).to_broadcast([2, FEAT]))
-            nc.scalar.dma_start(out=bias_rows[32:33, cols], in_=bias_in[1][half].unsqueeze(0))
-        for h in range(2):
-            nc.vector.memset(gate_rows[h][:].bitcast(I32), 0)
-            nc.vector.memset(gate_rows[h][0:32, :], 1.0)
-
-        def load_gate_rows(queue, h):
-            tokens = slice(h * (TOKENS // 2), (h + 1) * (TOKENS // 2))
-            queue.dma_start(
-                out=gate_rows[h][32:65:32, :], in_=gate_flat[tokens].unsqueeze(0).to_broadcast([2, TOKENS // 2])
-            )
-
-        load_gate_rows(nc.scalar, 0)
-
         x_sb = [keep.tile([P, GROUP, HID], BF16, name="x%d" % i) for i in range(GROUPS)]
         w_words = keep.tile([P, PASSES, 2, BANK], U32, name="w_words", align_bytes=64)
 
@@ -101,6 +82,14 @@ def tile_reasoningmultiheadattention_pa_t_kernel(
                     in_=words_in[side][half].rearrange("g p n t -> p g (n t)").bitcast(I32),
                 )
 
+        for side in range(2):
+            for half in range(2):
+                nc.scalar.dma_start(
+                    out=bias_rows[0:1, side, half * FEAT : (half + 1) * FEAT],
+                    in_=bias_in[side][half].unsqueeze(0),
+                )
+        m_bf = keep.tile([P, TILES], BF16, name="m_bf")
+        nc.scalar.dma_start(out=m_bf[:], in_=m_view)
         scale_pieces = [(side, half, quad) for side in (1, 0) for half in range(2) for quad in range(4)]
         load_x(0, 0, 2)
         load_scale_rows(scale_pieces[0:2])
@@ -112,7 +101,6 @@ def tile_reasoningmultiheadattention_pa_t_kernel(
         load_scale_rows(scale_pieces[8:12])
         load_words(0)
         load_scale_rows(scale_pieces[12:16])
-        load_gate_rows(nc.sync, 1)
         for i in range(2, GROUPS):
             load_x(i, 0, GROUP)
 
@@ -120,51 +108,44 @@ def tile_reasoningmultiheadattention_pa_t_kernel(
         planes = {}
         blended = {}
 
-        grouped = {}
-
-        def transpose_group(i):
+        def prepare(i):
             for j in range(GROUP):
                 t = i * GROUP + j
                 words = x_sb[i][:, j, :].bitcast(F32)
-                xt = psum_t.tile([P, PASSES, 2, P], F32, name="xt", tag="bank")
+                xt = psum.tile([P, PASSES, 2, P], F32, name="xt", tag="bank")
                 for g in range(PASSES):
                     for u in range(2):
                         nc.tensor.transpose(
                             xt[:, g, u, :], words[:, g * 256 + u : (g + 1) * 256 : 2], ident[:]
                         )
-                grouped[t] = ahead.tile([P, PASSES * P * 4], BF16, name="grouped", align_bytes=64)
+                grouped = stage.tile([P, PASSES * P * 4], BF16, name="grouped", align_bytes=64)
                 nc.scalar.copy(
-                    out=grouped[t][:].bitcast(F32).rearrange("p (g r u) -> p g r u", g=PASSES, u=2),
+                    out=grouped[:].bitcast(F32).rearrange("p (g r u) -> p g r u", g=PASSES, u=2),
                     in_=xt[:].rearrange("p g u r -> p g r u"),
                 )
+                codes[t] = ahead.tile([P, PASSES * P], U32, name="codes", align_bytes=64)
+                planes[t] = ahead.tile([P, PASSES * P], U8, name="planes", align_bytes=64)
+                nc.vector.quantize_mx(out=codes[t][:].bitcast(FP8X4), scales=planes[t][:], in_=grouped[:])
 
-        def quantise(t):
-            codes[t] = ahead.tile([P, PASSES * P], U32, name="codes", align_bytes=64)
-            planes[t] = ahead.tile([P, PASSES * P], U8, name="planes", align_bytes=64)
-            nc.vector.quantize_mx(out=codes[t][:].bitcast(FP8X4), scales=planes[t][:], in_=grouped[t][:])
+        def blend_biases_on_vector(i):
+            for t in range(i * GROUP, (i + 1) * GROUP):
+                blended[t] = ahead.tile([P, BANK], F32, name="blended")
+                nc.vector.scalar_tensor_tensor(
+                    out=blended[t][:], in0=bias_diff[:], scalar=m_f[:, t : t + 1], in1=bias_base[:],
+                    op0=MULT, op1=ADD,
+                )
 
-        def blend_biases(t):
-            blend_ps = psum_t.tile([P, BANK], F32, name="blend_ps", tag="bank")
-            nc.tensor.matmul(
-                out=blend_ps[:],
-                lhsT=gate_rows[t // (TILES // 2)][:, (t % (TILES // 2)) * P : (t % (TILES // 2) + 1) * P],
-                rhs=bias_rows[:],
-                start=True,
-                stop=True,
-            )
-            blended[t] = biases.tile([P, BANK], F32, name="blended")
-            if t < BLENDS_AHEAD and t % 2 == 1:
-                nc.vector.tensor_copy(out=blended[t][:], in_=blend_ps[:])
-            else:
-                nc.scalar.copy(out=blended[t][:], in_=blend_ps[:])
+        def blend_biases(i):
+            for t in range(i * GROUP, (i + 1) * GROUP):
+                blended[t] = ahead.tile([P, BANK], F32, name="blended")
+                nc.scalar.activation(out=blended[t][:], in_=bias_diff[:], func=COPY, scale=m_f[:, t : t + 1])
+                nc.gpsimd.tensor_tensor(out=blended[t][:], in0=blended[t][:], in1=bias_base[:], op=ADD)
 
         def project(i):
             for t in range(i * GROUP, (i + 1) * GROUP):
-                if t + BLENDS_AHEAD < TILES:
-                    blend_biases(t + BLENDS_AHEAD)
                 acc = [
-                    psum_mm.tile([P, BANK], F32, name="acc_base"),
-                    psum_mm.tile([P, BANK], F32, name="acc_reas"),
+                    psum.tile([P, BANK], F32, name="acc_base", tag="bank"),
+                    psum.tile([P, BANK], F32, name="acc_reas", tag="bank"),
                 ]
                 for side in (1, 0):
                     for g in range(PASSES):
@@ -182,8 +163,6 @@ def tile_reasoningmultiheadattention_pa_t_kernel(
                 nc.vector.scalar_tensor_tensor(
                     out=part[:], in0=acc[1][:], scalar=m_f[:, t : t + 1], in1=blended[t][:], op0=MULT, op1=ADD
                 )
-                if t + GROUP < TILES:
-                    quantise(t + GROUP)
                 result = stage.tile([P, BANK], F32, name="result")
                 nc.vector.scalar_tensor_tensor(
                     out=result[:], in0=acc[0][:], scalar=one_minus_m[:, t : t + 1], in1=part[:], op0=MULT, op1=ADD
@@ -191,22 +170,27 @@ def tile_reasoningmultiheadattention_pa_t_kernel(
                 for half in range(2):
                     nc.sync.dma_start(out=out_views[half][:, t, :], in_=result[:, half * FEAT : (half + 1) * FEAT])
 
-        transpose_group(0)
-        for t in range(GROUP):
-            quantise(t)
+        prepare(0)
 
-        nc.vector.tensor_scalar_mul(out=bias_rows[64:96, :], in0=bias_rows[64:96, :], scalar1=-1.0)
-        nc.vector.tensor_copy(out=gate_by_tile[0:TILES, :], in_=gate_by_tile_bf[:])
-        gate_ps = psum_t.tile([P, P], F32, name="gate_ps", tag="bank")
-        nc.tensor.transpose(gate_ps[:], gate_by_tile[:], ident[:])
         m_f = keep.tile([P, TILES], F32, name="m_f")
-        nc.vector.tensor_copy(out=m_f[:], in_=gate_ps[:, 0:TILES])
+        nc.vector.tensor_copy(out=m_f[:], in_=m_bf[:])
         one_minus_m = keep.tile([P, TILES], F32, name="one_minus_m")
         nc.vector.tensor_scalar(out=one_minus_m[:], in0=m_f[:], scalar1=-1.0, scalar2=1.0, op0=MULT, op1=ADD)
+        base_ps = psum.tile([P, BANK], F32, name="base_ps", tag="bank")
+        nc.tensor.matmul(out=base_ps[:], lhsT=ones[:], rhs=bias_rows[:, 0, :], start=True, stop=True)
+        reas_ps = psum.tile([P, BANK], F32, name="reas_ps", tag="bank")
+        nc.tensor.matmul(out=reas_ps[:], lhsT=ones[:], rhs=bias_rows[:, 1, :], start=True, stop=True)
+        bias_base = keep.tile([P, BANK], F32, name="bias_base")
+        nc.vector.tensor_copy(out=bias_base[:], in_=base_ps[:])
+        bias_diff = keep.tile([P, BANK], F32, name="bias_diff")
+        nc.vector.tensor_tensor(out=bias_diff[:], in0=reas_ps[:], in1=bias_base[:], op=SUBTRACT)
 
-        for t in range(BLENDS_AHEAD):
-            blend_biases(t)
+        blend_biases_on_vector(0)
+        for i in range(1, LOOKAHEAD):
+            prepare(i)
         for i in range(GROUPS):
+            if i + LOOKAHEAD < GROUPS:
+                prepare(i + LOOKAHEAD)
             if i + 1 < GROUPS:
-                transpose_group(i + 1)
+                blend_biases(i + 1)
             project(i)

@@ -11,8 +11,6 @@ U8 = mybir.dt.uint8
 FP8X4 = mybir.dt.float8_e4m3fn_x4
 MULT = mybir.AluOpType.mult
 ADD = mybir.AluOpType.add
-SUBTRACT = mybir.AluOpType.subtract
-COPY = mybir.ActivationFunctionType.Copy
 
 P = 128
 TOKENS = 4096
@@ -24,7 +22,7 @@ BANK = 2 * FEAT
 TILES = TOKENS // P
 GROUP = 4
 GROUPS = TILES // GROUP
-LOOKAHEAD = 1
+BLENDS_AHEAD = 4
 
 FLOPS = 2 * TOKENS * HID * 4 * FEAT
 
@@ -36,10 +34,10 @@ def tile_reasoningmultiheadattention_pa_t_kernel(
     out_0, out_1,
 ):
     nc = tc.nc
-    x_view = x.rearrange("b s k -> (b s) k").rearrange("(p t) k -> p t k", t=TILES)
-    m_view = reasoning_mask.rearrange("b s o i -> (b s o i)").rearrange("(p t) -> p t", t=TILES)
+    x_view = x.rearrange("b s k -> (b s) k").rearrange("(t p) k -> p t k", p=P)
+    gate_flat = reasoning_mask.rearrange("b s o i -> (b s o i)")
     out_views = [
-        o.rearrange("b s h d -> (b s) (h d)").rearrange("(p t) n -> p t n", t=TILES) for o in (out_0, out_1)
+        o.rearrange("b s h d -> (b s) (h d)").rearrange("(t p) n -> p t n", p=P) for o in (out_0, out_1)
     ]
     words_in = [[Wq_words, Wk_words], [Wqr_words, Wkr_words]]
     scales_in = [[Wq_scales, Wk_scales], [Wqr_scales, Wkr_scales]]
@@ -49,17 +47,29 @@ def tile_reasoningmultiheadattention_pa_t_kernel(
         ctx.enter_context(tc.manual_schedule())
         keep = ctx.enter_context(tc.tile_pool(name="keep", bufs=1))
         stage = ctx.enter_context(tc.tile_pool(name="stage", bufs=6))
-        ahead = ctx.enter_context(tc.tile_pool(name="ahead", bufs=(LOOKAHEAD + 1) * GROUP))
+        ahead = ctx.enter_context(tc.tile_pool(name="ahead", bufs=2 * GROUP))
+        biases = ctx.enter_context(tc.tile_pool(name="biases", bufs=BLENDS_AHEAD + 2))
         psum = ctx.enter_context(tc.psum_pool(name="psum", bufs=8))
 
-        w_planes = keep.tile([P, BANK], U8, name="w_planes", align_bytes=64)
-        nc.vector.memset(w_planes[:].bitcast(I32), 0)
         ident = keep.tile([P, P], F32, name="ident")
         make_identity(nc, ident[:])
-        ones = keep.tile([P, P], BF16, name="ones")
-        nc.vector.memset(ones[:], 1.0)
-        bias_rows = keep.tile([P, 2, BANK], BF16, name="bias_rows")
+        w_planes = keep.tile([P, BANK], U8, name="w_planes", align_bytes=64)
+        nc.vector.memset(w_planes[:].bitcast(I32), 0)
+        bias_rows = keep.tile([P, BANK], BF16, name="bias_rows")
         nc.vector.memset(bias_rows[:], 0.0)
+        gate_by_tile = keep.tile([P, P], F32, name="gate_by_tile")
+        nc.vector.memset(gate_by_tile[:], 0.0)
+        gate_rows = keep.tile([P, TOKENS], BF16, name="gate_rows")
+        gate_by_tile_bf = keep.tile([TILES, P], BF16, name="gate_by_tile_bf")
+        nc.scalar.dma_start(out=gate_by_tile_bf[:], in_=gate_flat.rearrange("(t p) -> t p", p=P))
+        for half in range(2):
+            cols = slice(half * FEAT, (half + 1) * FEAT)
+            nc.scalar.dma_start(out=bias_rows[0:P:64, cols], in_=bias_in[0][half].unsqueeze(0).to_broadcast([2, FEAT]))
+            nc.scalar.dma_start(out=bias_rows[32:33, cols], in_=bias_in[1][half].unsqueeze(0))
+        nc.vector.memset(gate_rows[:].bitcast(I32), 0)
+        nc.vector.memset(gate_rows[0:32, :], 1.0)
+        nc.gpsimd.dma_start(out=gate_rows[32:65:32, :], in_=gate_flat.unsqueeze(0).to_broadcast([2, TOKENS]))
+
         x_sb = [keep.tile([P, GROUP, HID], BF16, name="x%d" % i) for i in range(GROUPS)]
         w_words = keep.tile([P, PASSES, 2, BANK], U32, name="w_words", align_bytes=64)
 
@@ -82,14 +92,6 @@ def tile_reasoningmultiheadattention_pa_t_kernel(
                     in_=words_in[side][half].rearrange("g p n t -> p g (n t)").bitcast(I32),
                 )
 
-        for side in range(2):
-            for half in range(2):
-                nc.scalar.dma_start(
-                    out=bias_rows[0:1, side, half * FEAT : (half + 1) * FEAT],
-                    in_=bias_in[side][half].unsqueeze(0),
-                )
-        m_bf = keep.tile([P, TILES], BF16, name="m_bf")
-        nc.scalar.dma_start(out=m_bf[:], in_=m_view)
         scale_pieces = [(side, half, quad) for side in (1, 0) for half in range(2) for quad in range(4)]
         load_x(0, 0, 2)
         load_scale_rows(scale_pieces[0:2])
@@ -108,7 +110,9 @@ def tile_reasoningmultiheadattention_pa_t_kernel(
         planes = {}
         blended = {}
 
-        def prepare(i):
+        grouped = {}
+
+        def transpose_group(i):
             for j in range(GROUP):
                 t = i * GROUP + j
                 words = x_sb[i][:, j, :].bitcast(F32)
@@ -118,31 +122,33 @@ def tile_reasoningmultiheadattention_pa_t_kernel(
                         nc.tensor.transpose(
                             xt[:, g, u, :], words[:, g * 256 + u : (g + 1) * 256 : 2], ident[:]
                         )
-                grouped = stage.tile([P, PASSES * P * 4], BF16, name="grouped", align_bytes=64)
+                grouped[t] = ahead.tile([P, PASSES * P * 4], BF16, name="grouped", align_bytes=64)
                 nc.scalar.copy(
-                    out=grouped[:].bitcast(F32).rearrange("p (g r u) -> p g r u", g=PASSES, u=2),
+                    out=grouped[t][:].bitcast(F32).rearrange("p (g r u) -> p g r u", g=PASSES, u=2),
                     in_=xt[:].rearrange("p g u r -> p g r u"),
                 )
-                codes[t] = ahead.tile([P, PASSES * P], U32, name="codes", align_bytes=64)
-                planes[t] = ahead.tile([P, PASSES * P], U8, name="planes", align_bytes=64)
-                nc.vector.quantize_mx(out=codes[t][:].bitcast(FP8X4), scales=planes[t][:], in_=grouped[:])
 
-        def blend_biases_on_vector(i):
-            for t in range(i * GROUP, (i + 1) * GROUP):
-                blended[t] = ahead.tile([P, BANK], F32, name="blended")
-                nc.vector.scalar_tensor_tensor(
-                    out=blended[t][:], in0=bias_diff[:], scalar=m_f[:, t : t + 1], in1=bias_base[:],
-                    op0=MULT, op1=ADD,
-                )
+        def quantise(t):
+            codes[t] = ahead.tile([P, PASSES * P], U32, name="codes", align_bytes=64)
+            planes[t] = ahead.tile([P, PASSES * P], U8, name="planes", align_bytes=64)
+            nc.vector.quantize_mx(out=codes[t][:].bitcast(FP8X4), scales=planes[t][:], in_=grouped[t][:])
 
-        def blend_biases(i):
-            for t in range(i * GROUP, (i + 1) * GROUP):
-                blended[t] = ahead.tile([P, BANK], F32, name="blended")
-                nc.scalar.activation(out=blended[t][:], in_=bias_diff[:], func=COPY, scale=m_f[:, t : t + 1])
-                nc.gpsimd.tensor_tensor(out=blended[t][:], in0=blended[t][:], in1=bias_base[:], op=ADD)
+        def blend_biases(t):
+            blend_ps = psum.tile([P, BANK], F32, name="blend_ps", tag="bank")
+            nc.tensor.matmul(
+                out=blend_ps[:],
+                lhsT=gate_rows[:, t * P : (t + 1) * P],
+                rhs=bias_rows[:],
+                start=True,
+                stop=True,
+            )
+            blended[t] = biases.tile([P, BANK], F32, name="blended")
+            nc.scalar.copy(out=blended[t][:], in_=blend_ps[:])
 
         def project(i):
             for t in range(i * GROUP, (i + 1) * GROUP):
+                if t + BLENDS_AHEAD < TILES:
+                    blend_biases(t + BLENDS_AHEAD)
                 acc = [
                     psum.tile([P, BANK], F32, name="acc_base", tag="bank"),
                     psum.tile([P, BANK], F32, name="acc_reas", tag="bank"),
@@ -163,6 +169,8 @@ def tile_reasoningmultiheadattention_pa_t_kernel(
                 nc.vector.scalar_tensor_tensor(
                     out=part[:], in0=acc[1][:], scalar=m_f[:, t : t + 1], in1=blended[t][:], op0=MULT, op1=ADD
                 )
+                if t + GROUP < TILES:
+                    quantise(t + GROUP)
                 result = stage.tile([P, BANK], F32, name="result")
                 nc.vector.scalar_tensor_tensor(
                     out=result[:], in0=acc[0][:], scalar=one_minus_m[:, t : t + 1], in1=part[:], op0=MULT, op1=ADD
@@ -170,27 +178,23 @@ def tile_reasoningmultiheadattention_pa_t_kernel(
                 for half in range(2):
                     nc.sync.dma_start(out=out_views[half][:, t, :], in_=result[:, half * FEAT : (half + 1) * FEAT])
 
-        prepare(0)
+        transpose_group(0)
 
+        nc.vector.tensor_scalar_mul(out=bias_rows[64:96, :], in0=bias_rows[64:96, :], scalar1=-1.0)
+        nc.vector.tensor_copy(out=gate_by_tile[0:TILES, :], in_=gate_by_tile_bf[:])
+        gate_ps = psum.tile([P, P], F32, name="gate_ps", tag="bank")
+        nc.tensor.transpose(gate_ps[:], gate_by_tile[:], ident[:])
         m_f = keep.tile([P, TILES], F32, name="m_f")
-        nc.vector.tensor_copy(out=m_f[:], in_=m_bf[:])
+        nc.vector.tensor_copy(out=m_f[:], in_=gate_ps[:, 0:TILES])
         one_minus_m = keep.tile([P, TILES], F32, name="one_minus_m")
         nc.vector.tensor_scalar(out=one_minus_m[:], in0=m_f[:], scalar1=-1.0, scalar2=1.0, op0=MULT, op1=ADD)
-        base_ps = psum.tile([P, BANK], F32, name="base_ps", tag="bank")
-        nc.tensor.matmul(out=base_ps[:], lhsT=ones[:], rhs=bias_rows[:, 0, :], start=True, stop=True)
-        reas_ps = psum.tile([P, BANK], F32, name="reas_ps", tag="bank")
-        nc.tensor.matmul(out=reas_ps[:], lhsT=ones[:], rhs=bias_rows[:, 1, :], start=True, stop=True)
-        bias_base = keep.tile([P, BANK], F32, name="bias_base")
-        nc.vector.tensor_copy(out=bias_base[:], in_=base_ps[:])
-        bias_diff = keep.tile([P, BANK], F32, name="bias_diff")
-        nc.vector.tensor_tensor(out=bias_diff[:], in0=reas_ps[:], in1=bias_base[:], op=SUBTRACT)
 
-        blend_biases_on_vector(0)
-        for i in range(1, LOOKAHEAD):
-            prepare(i)
+        for t in range(GROUP):
+            quantise(t)
+        transpose_group(1)
+        for t in range(BLENDS_AHEAD):
+            blend_biases(t)
         for i in range(GROUPS):
-            if i + LOOKAHEAD < GROUPS:
-                prepare(i + LOOKAHEAD)
-            if i + 1 < GROUPS:
-                blend_biases(i + 1)
             project(i)
+            if i + 2 < GROUPS:
+                transpose_group(i + 2)

@@ -49,6 +49,7 @@ def tile_reasoningmultiheadattention_pa_t_kernel(
         stage = ctx.enter_context(tc.tile_pool(name="stage", bufs=6))
         ahead = ctx.enter_context(tc.tile_pool(name="ahead", bufs=2 * GROUP))
         biases = ctx.enter_context(tc.tile_pool(name="biases", bufs=BLENDS_AHEAD + 2))
+        sorted_pool = ctx.enter_context(tc.tile_pool(name="sorted_pool", bufs=3 * GROUP))
         psum = ctx.enter_context(tc.psum_pool(name="psum", bufs=8))
 
         ident = keep.tile([P, P], F32, name="ident")
@@ -111,17 +112,22 @@ def tile_reasoningmultiheadattention_pa_t_kernel(
         blended = {}
 
         grouped = {}
+        sorted_words = {}
+
+        def sort_words(t):
+            words = x_sb[t // GROUP][:, t % GROUP, :].bitcast(F32)
+            sorted_words[t] = sorted_pool.tile([P, PASSES, 2, P], F32, name="sorted_words")
+            nc.scalar.copy(
+                out=sorted_words[t][:], in_=words.rearrange("p (g r u) -> p g u r", g=PASSES, u=2)
+            )
 
         def transpose_group(i):
             for j in range(GROUP):
                 t = i * GROUP + j
-                words = x_sb[i][:, j, :].bitcast(F32)
                 xt = psum.tile([P, PASSES, 2, P], F32, name="xt", tag="bank")
                 for g in range(PASSES):
                     for u in range(2):
-                        nc.tensor.transpose(
-                            xt[:, g, u, :], words[:, g * 256 + u : (g + 1) * 256 : 2], ident[:]
-                        )
+                        nc.tensor.transpose(xt[:, g, u, :], sorted_words[t][:, g, u, :], ident[:])
                 grouped[t] = ahead.tile([P, PASSES * P * 4], BF16, name="grouped", align_bytes=64)
                 nc.scalar.copy(
                     out=grouped[t][:].bitcast(F32).rearrange("p (g r u) -> p g r u", g=PASSES, u=2),
@@ -149,6 +155,8 @@ def tile_reasoningmultiheadattention_pa_t_kernel(
             for t in range(i * GROUP, (i + 1) * GROUP):
                 if t + BLENDS_AHEAD < TILES:
                     blend_biases(t + BLENDS_AHEAD)
+                if t + 3 * GROUP < TILES:
+                    sort_words(t + 3 * GROUP)
                 acc = [
                     psum.tile([P, BANK], F32, name="acc_base", tag="bank"),
                     psum.tile([P, BANK], F32, name="acc_reas", tag="bank"),
@@ -178,6 +186,8 @@ def tile_reasoningmultiheadattention_pa_t_kernel(
                 for half in range(2):
                     nc.sync.dma_start(out=out_views[half][:, t, :], in_=result[:, half * FEAT : (half + 1) * FEAT])
 
+        for t in range(GROUP):
+            sort_words(t)
         transpose_group(0)
 
         nc.vector.tensor_scalar_mul(out=bias_rows[64:96, :], in0=bias_rows[64:96, :], scalar1=-1.0)
@@ -189,11 +199,15 @@ def tile_reasoningmultiheadattention_pa_t_kernel(
         one_minus_m = keep.tile([P, TILES], F32, name="one_minus_m")
         nc.vector.tensor_scalar(out=one_minus_m[:], in0=m_f[:], scalar1=-1.0, scalar2=1.0, op0=MULT, op1=ADD)
 
+        for t in range(GROUP, 2 * GROUP):
+            sort_words(t)
         for t in range(GROUP):
             quantise(t)
         transpose_group(1)
         for t in range(BLENDS_AHEAD):
             blend_biases(t)
+        for t in range(2 * GROUP, 3 * GROUP):
+            sort_words(t)
         for i in range(GROUPS):
             project(i)
             if i + 2 < GROUPS:

@@ -49,7 +49,7 @@ def tile_reasoningmultiheadattention_pa_t_kernel(
         stage = ctx.enter_context(tc.tile_pool(name="stage", bufs=6))
         ahead = ctx.enter_context(tc.tile_pool(name="ahead", bufs=2 * GROUP))
         biases = ctx.enter_context(tc.tile_pool(name="biases", bufs=BLENDS_AHEAD + 2))
-        sorted_pool = ctx.enter_context(tc.tile_pool(name="sorted_pool", bufs=3 * GROUP))
+        sorted_pool = ctx.enter_context(tc.tile_pool(name="sorted_pool", bufs=2 * GROUP))
         psum = ctx.enter_context(tc.psum_pool(name="psum", bufs=8))
 
         ident = keep.tile([P, P], F32, name="ident")
@@ -127,7 +127,13 @@ def tile_reasoningmultiheadattention_pa_t_kernel(
                 xt = psum.tile([P, PASSES, 2, P], F32, name="xt", tag="bank")
                 for g in range(PASSES):
                     for u in range(2):
-                        nc.tensor.transpose(xt[:, g, u, :], sorted_words[t][:, g, u, :], ident[:])
+                        if t in sorted_words:
+                            nc.tensor.transpose(xt[:, g, u, :], sorted_words[t][:, g, u, :], ident[:])
+                        else:
+                            words = x_sb[i][:, j, :].bitcast(F32)
+                            nc.tensor.transpose(
+                                xt[:, g, u, :], words[:, g * 256 + u : (g + 1) * 256 : 2], ident[:]
+                            )
                 grouped[t] = ahead.tile([P, PASSES * P * 4], BF16, name="grouped", align_bytes=64)
                 nc.scalar.copy(
                     out=grouped[t][:].bitcast(F32).rearrange("p (g r u) -> p g r u", g=PASSES, u=2),
@@ -153,10 +159,10 @@ def tile_reasoningmultiheadattention_pa_t_kernel(
 
         def project(i):
             for t in range(i * GROUP, (i + 1) * GROUP):
+                if t + 2 * GROUP < TILES:
+                    sort_words(t + 2 * GROUP)
                 if t + BLENDS_AHEAD < TILES:
                     blend_biases(t + BLENDS_AHEAD)
-                if t + 3 * GROUP < TILES:
-                    sort_words(t + 3 * GROUP)
                 acc = [
                     psum.tile([P, BANK], F32, name="acc_base", tag="bank"),
                     psum.tile([P, BANK], F32, name="acc_reas", tag="bank"),
@@ -186,8 +192,6 @@ def tile_reasoningmultiheadattention_pa_t_kernel(
                 for half in range(2):
                     nc.sync.dma_start(out=out_views[half][:, t, :], in_=result[:, half * FEAT : (half + 1) * FEAT])
 
-        for t in range(GROUP):
-            sort_words(t)
         transpose_group(0)
 
         nc.vector.tensor_scalar_mul(out=bias_rows[64:96, :], in0=bias_rows[64:96, :], scalar1=-1.0)
@@ -199,15 +203,11 @@ def tile_reasoningmultiheadattention_pa_t_kernel(
         one_minus_m = keep.tile([P, TILES], F32, name="one_minus_m")
         nc.vector.tensor_scalar(out=one_minus_m[:], in0=m_f[:], scalar1=-1.0, scalar2=1.0, op0=MULT, op1=ADD)
 
-        for t in range(GROUP, 2 * GROUP):
-            sort_words(t)
         for t in range(GROUP):
             quantise(t)
         transpose_group(1)
         for t in range(BLENDS_AHEAD):
             blend_biases(t)
-        for t in range(2 * GROUP, 3 * GROUP):
-            sort_words(t)
         for i in range(GROUPS):
             project(i)
             if i + 2 < GROUPS:

@@ -22,6 +22,7 @@ BANK = 2 * FEAT
 TILES = TOKENS // P
 GROUP = 4
 GROUPS = TILES // GROUP
+RESULTS_WAITING = 16
 BLENDS_AHEAD = 4
 
 FLOPS = 2 * TOKENS * HID * 4 * FEAT
@@ -46,7 +47,8 @@ def tile_reasoningmultiheadattention_pa_t_kernel(
     with ExitStack() as ctx:
         ctx.enter_context(tc.manual_schedule())
         keep = ctx.enter_context(tc.tile_pool(name="keep", bufs=1))
-        stage = ctx.enter_context(tc.tile_pool(name="stage", bufs=6))
+        stage = ctx.enter_context(tc.tile_pool(name="stage", bufs=4))
+        results = ctx.enter_context(tc.tile_pool(name="results", bufs=RESULTS_WAITING))
         ahead = ctx.enter_context(tc.tile_pool(name="ahead", bufs=2 * GROUP))
         biases = ctx.enter_context(tc.tile_pool(name="biases", bufs=BLENDS_AHEAD + 2))
         sorted_pool = ctx.enter_context(tc.tile_pool(name="sorted_pool", bufs=2 * GROUP))
@@ -67,9 +69,12 @@ def tile_reasoningmultiheadattention_pa_t_kernel(
             cols = slice(half * FEAT, (half + 1) * FEAT)
             nc.scalar.dma_start(out=bias_rows[0:P:64, cols], in_=bias_in[0][half].unsqueeze(0).to_broadcast([2, FEAT]))
             nc.scalar.dma_start(out=bias_rows[32:33, cols], in_=bias_in[1][half].unsqueeze(0))
-        nc.vector.memset(gate_rows[:].bitcast(I32), 0)
-        nc.vector.memset(gate_rows[0:32, :], 1.0)
-        nc.gpsimd.dma_start(out=gate_rows[32:65:32, :], in_=gate_flat.unsqueeze(0).to_broadcast([2, TOKENS]))
+        for queue, first, last in ((nc.scalar, 0, 2 * GROUP * P), (nc.gpsimd, 2 * GROUP * P, TOKENS)):
+            nc.vector.memset(gate_rows[:, first:last], 1.0)
+            queue.dma_start(
+                out=gate_rows[32:65:32, first:last],
+                in_=gate_flat[first:last].unsqueeze(0).to_broadcast([2, last - first]),
+            )
 
         x_sb = [keep.tile([P, GROUP, HID], BF16, name="x%d" % i) for i in range(GROUPS)]
         w_words = keep.tile([P, PASSES, 2, BANK], U32, name="w_words", align_bytes=64)
@@ -94,17 +99,22 @@ def tile_reasoningmultiheadattention_pa_t_kernel(
                 )
 
         scale_pieces = [(side, half, quad) for side in (1, 0) for half in range(2) for quad in range(4)]
-        load_x(0, 0, 2)
+        load_x(0, 0, 1)
+        load_x(0, 1, 1)
         load_scale_rows(scale_pieces[0:2])
         load_x(0, 2, 2)
         load_scale_rows(scale_pieces[2:4])
-        load_x(1, 0, GROUP)
-        load_scale_rows(scale_pieces[4:8])
+        load_x(1, 0, 2)
+        load_scale_rows(scale_pieces[4:6])
+        load_x(1, 2, 2)
+        load_scale_rows(scale_pieces[6:8])
         load_words(1)
         load_scale_rows(scale_pieces[8:12])
         load_words(0)
         load_scale_rows(scale_pieces[12:16])
-        for i in range(2, GROUPS):
+        load_x(2, 0, 2)
+        load_x(2, 2, 2)
+        for i in range(3, GROUPS):
             load_x(i, 0, GROUP)
 
         codes = {}
@@ -185,7 +195,7 @@ def tile_reasoningmultiheadattention_pa_t_kernel(
                 )
                 if t + GROUP < TILES:
                     quantise(t + GROUP)
-                result = stage.tile([P, BANK], F32, name="result")
+                result = results.tile([P, BANK], F32, name="result")
                 nc.vector.scalar_tensor_tensor(
                     out=result[:], in0=acc[0][:], scalar=one_minus_m[:, t : t + 1], in1=part[:], op0=MULT, op1=ADD
                 )

@@ -75,6 +75,11 @@ def tile_reasoningmultiheadattention_pa_t_kernel(
                 out=gate_rows[32:65:32, first:last],
                 in_=gate_flat[first:last].unsqueeze(0).to_broadcast([2, last - first]),
             )
+        pick = keep.tile([P, 2 * P], BF16, name="pick")
+        nc.vector.memset(pick[:], 0.0)
+        nc.vector.memset(pick[0:32, 0:P], 1.0)
+        nc.vector.memset(pick[32:64, P : 2 * P], 1.0)
+        nc.vector.memset(pick[64:96, P : 2 * P], 1.0)
 
         x_sb = [keep.tile([P, GROUP, HID], BF16, name="x%d" % i) for i in range(GROUPS)]
         w_words = keep.tile([P, PASSES, 2, BANK], U32, name="w_words", align_bytes=64)
@@ -167,11 +172,17 @@ def tile_reasoningmultiheadattention_pa_t_kernel(
             blended[t] = biases.tile([P, BANK], F32, name="blended")
             nc.scalar.copy(out=blended[t][:], in_=blend_ps[:])
 
+        def blend_biases_on_vector(t):
+            blended[t] = biases.tile([P, BANK], F32, name="blended")
+            nc.vector.scalar_tensor_tensor(
+                out=blended[t][:], in0=bias_step[:], scalar=m_f[:, t : t + 1], in1=bias_base[:], op0=MULT, op1=ADD
+            )
+
         def project(i):
             for t in range(i * GROUP, (i + 1) * GROUP):
                 if t + 2 * GROUP < TILES:
                     sort_words(t + 2 * GROUP)
-                if t + BLENDS_AHEAD < TILES:
+                if t + BLENDS_AHEAD < TILES and (t + BLENDS_AHEAD) % GROUP != GROUP - 1:
                     blend_biases(t + BLENDS_AHEAD)
                 acc = [
                     psum.tile([P, BANK], F32, name="acc_base", tag="bank"),
@@ -201,6 +212,8 @@ def tile_reasoningmultiheadattention_pa_t_kernel(
                 )
                 for half in range(2):
                     nc.sync.dma_start(out=out_views[half][:, t, :], in_=result[:, half * FEAT : (half + 1) * FEAT])
+            if i + 1 < GROUPS:
+                blend_biases_on_vector((i + 2) * GROUP - 1)
 
         transpose_group(0)
 
@@ -216,8 +229,16 @@ def tile_reasoningmultiheadattention_pa_t_kernel(
         for t in range(GROUP):
             quantise(t)
         transpose_group(1)
-        for t in range(BLENDS_AHEAD):
+        spread = []
+        for c in range(2):
+            spread_ps = psum.tile([P, BANK], F32, name="spread_ps", tag="bank")
+            nc.tensor.matmul(out=spread_ps[:], lhsT=pick[:, c * P : (c + 1) * P], rhs=bias_rows[:], start=True, stop=True)
+            spread.append(keep.tile([P, BANK], F32, name="spread%d" % c))
+            nc.vector.tensor_copy(out=spread[c][:], in_=spread_ps[:])
+        bias_base, bias_step = spread
+        for t in range(GROUP - 1):
             blend_biases(t)
+        blend_biases_on_vector(GROUP - 1)
         for i in range(GROUPS):
             project(i)
             if i + 2 < GROUPS:

@@ -11,6 +11,7 @@ U8 = mybir.dt.uint8
 FP8X4 = mybir.dt.float8_e4m3fn_x4
 MULT = mybir.AluOpType.mult
 ADD = mybir.AluOpType.add
+COPY = mybir.ActivationFunctionType.Copy
 
 P = 128
 TOKENS = 4096
@@ -172,6 +173,9 @@ def tile_reasoningmultiheadattention_pa_t_kernel(
             blended[t] = biases.tile([P, BANK], F32, name="blended")
             nc.scalar.copy(out=blended[t][:], in_=blend_ps[:])
 
+        def blended_by_vector(t):
+            return t % GROUP == GROUP - 1 and t < TILES - 1
+
         def blend_biases_on_vector(t):
             blended[t] = biases.tile([P, BANK], F32, name="blended")
             nc.vector.scalar_tensor_tensor(
@@ -182,7 +186,7 @@ def tile_reasoningmultiheadattention_pa_t_kernel(
             for t in range(i * GROUP, (i + 1) * GROUP):
                 if t + 2 * GROUP < TILES:
                     sort_words(t + 2 * GROUP)
-                if t + BLENDS_AHEAD < TILES and (t + BLENDS_AHEAD) % GROUP != GROUP - 1:
+                if t + BLENDS_AHEAD < TILES and not blended_by_vector(t + BLENDS_AHEAD):
                     blend_biases(t + BLENDS_AHEAD)
                 acc = [
                     psum.tile([P, BANK], F32, name="acc_base", tag="bank"),
@@ -207,12 +211,17 @@ def tile_reasoningmultiheadattention_pa_t_kernel(
                 if t + GROUP < TILES:
                     quantise(t + GROUP)
                 result = results.tile([P, BANK], F32, name="result")
-                nc.vector.scalar_tensor_tensor(
-                    out=result[:], in0=acc[0][:], scalar=one_minus_m[:, t : t + 1], in1=part[:], op0=MULT, op1=ADD
-                )
+                if t % GROUP == 1:
+                    scaled = stage.tile([P, BANK], F32, name="scaled")
+                    nc.scalar.activation(out=scaled[:], in_=acc[0][:], func=COPY, scale=one_minus_m[:, t : t + 1])
+                    nc.gpsimd.tensor_tensor(out=result[:], in0=scaled[:], in1=part[:], op=ADD)
+                else:
+                    nc.vector.scalar_tensor_tensor(
+                        out=result[:], in0=acc[0][:], scalar=one_minus_m[:, t : t + 1], in1=part[:], op0=MULT, op1=ADD
+                    )
                 for half in range(2):
                     nc.sync.dma_start(out=out_views[half][:, t, :], in_=result[:, half * FEAT : (half + 1) * FEAT])
-            if i + 1 < GROUPS:
+            if blended_by_vector((i + 2) * GROUP - 1):
                 blend_biases_on_vector((i + 2) * GROUP - 1)
 
         transpose_group(0)

@@ -24,6 +24,7 @@ TILES = TOKENS // P
 GROUP = 4
 GROUPS = TILES // GROUP
 RESULTS_WAITING = 16
+EARLY_BLENDS = range(GROUP + 2, TILES - GROUP, GROUP)
 BLENDS_AHEAD = 4
 
 FLOPS = 2 * TOKENS * HID * 4 * FEAT
@@ -137,9 +138,9 @@ def tile_reasoningmultiheadattention_pa_t_kernel(
                 out=sorted_words[t][:], in_=words.rearrange("p (g r u) -> p g u r", g=PASSES, u=2)
             )
 
-        def transpose_group(i):
-            for j in range(GROUP):
-                t = i * GROUP + j
+        def transpose_tiles(tiles):
+            for t in tiles:
+                i, j = divmod(t, GROUP)
                 xt = psum.tile([P, PASSES, 2, P], F32, name="xt", tag="bank")
                 for g in range(PASSES):
                     for u in range(2):
@@ -174,57 +175,76 @@ def tile_reasoningmultiheadattention_pa_t_kernel(
             nc.scalar.copy(out=blended[t][:], in_=blend_ps[:])
 
         def blended_by_vector(t):
-            return t % GROUP == GROUP - 1 and t < TILES - 1
+            return (t % GROUP == GROUP - 1 and t < TILES - 1) or t in EARLY_BLENDS
 
         def blend_biases_on_vector(t):
-            blended[t] = biases.tile([P, BANK], F32, name="blended")
+            if t in EARLY_BLENDS:
+                blended[t] = keep.tile([P, BANK], F32, name="early%d" % t)
+            else:
+                blended[t] = biases.tile([P, BANK], F32, name="blended")
             nc.vector.scalar_tensor_tensor(
                 out=blended[t][:], in0=bias_step[:], scalar=m_f[:, t : t + 1], in1=bias_base[:], op0=MULT, op1=ADD
             )
 
-        def project(i):
-            for t in range(i * GROUP, (i + 1) * GROUP):
-                if t + 2 * GROUP < TILES:
-                    sort_words(t + 2 * GROUP)
-                if t + BLENDS_AHEAD < TILES and not blended_by_vector(t + BLENDS_AHEAD):
-                    blend_biases(t + BLENDS_AHEAD)
-                acc = [
-                    psum.tile([P, BANK], F32, name="acc_base", tag="bank"),
-                    psum.tile([P, BANK], F32, name="acc_reas", tag="bank"),
-                ]
-                for side in (1, 0):
-                    for g in range(PASSES):
-                        first = 8 * side + 4 * g
-                        nc.tensor.matmul_mx(
-                            out=acc[side][:],
-                            lhsT=codes[t][:, g * P : (g + 1) * P].bitcast(FP8X4),
-                            lhsT_scale=planes[t][:, g * P : (g + 1) * P],
-                            rhs=w_words[:, g, side, :].bitcast(FP8X4),
-                            rhs_scale=w_planes[first:P, :],
-                            start=(g == 0),
-                            stop=(g == PASSES - 1),
-                        )
-                part = stage.tile([P, BANK], F32, name="part")
-                nc.vector.scalar_tensor_tensor(
-                    out=part[:], in0=acc[1][:], scalar=m_f[:, t : t + 1], in1=blended[t][:], op0=MULT, op1=ADD
+        acc = {}
+        parts = {}
+
+        def multiply(t, side):
+            acc[t, side] = psum.tile([P, BANK], F32, name="acc%d" % side, tag="bank")
+            for g in range(PASSES):
+                first = 8 * side + 4 * g
+                nc.tensor.matmul_mx(
+                    out=acc[t, side][:],
+                    lhsT=codes[t][:, g * P : (g + 1) * P].bitcast(FP8X4),
+                    lhsT_scale=planes[t][:, g * P : (g + 1) * P],
+                    rhs=w_words[:, g, side, :].bitcast(FP8X4),
+                    rhs_scale=w_planes[first:P, :],
+                    start=(g == 0),
+                    stop=(g == PASSES - 1),
                 )
-                if t + GROUP < TILES:
-                    quantise(t + GROUP)
-                result = results.tile([P, BANK], F32, name="result")
-                if t % GROUP == 1:
-                    scaled = stage.tile([P, BANK], F32, name="scaled")
-                    nc.scalar.activation(out=scaled[:], in_=acc[0][:], func=COPY, scale=one_minus_m[:, t : t + 1])
-                    nc.gpsimd.tensor_tensor(out=result[:], in0=scaled[:], in1=part[:], op=ADD)
-                else:
-                    nc.vector.scalar_tensor_tensor(
-                        out=result[:], in0=acc[0][:], scalar=one_minus_m[:, t : t + 1], in1=part[:], op0=MULT, op1=ADD
-                    )
-                for half in range(2):
-                    nc.sync.dma_start(out=out_views[half][:, t, :], in_=result[:, half * FEAT : (half + 1) * FEAT])
-            if blended_by_vector((i + 2) * GROUP - 1):
+
+        def reasoning_side(t):
+            if t + 2 * GROUP < TILES:
+                sort_words(t + 2 * GROUP)
+            if t + BLENDS_AHEAD < TILES and not blended_by_vector(t + BLENDS_AHEAD):
+                blend_biases(t + BLENDS_AHEAD)
+            multiply(t, 1)
+            parts[t] = stage.tile([P, BANK], F32, name="part")
+            nc.vector.scalar_tensor_tensor(
+                out=parts[t][:], in0=acc[t, 1][:], scalar=m_f[:, t : t + 1], in1=blended[t][:], op0=MULT, op1=ADD
+            )
+            if t + GROUP < TILES:
+                quantise(t + GROUP)
+
+        def base_side(t):
+            multiply(t, 0)
+            result = results.tile([P, BANK], F32, name="result")
+            if t % GROUP == 1:
+                scaled = stage.tile([P, BANK], F32, name="scaled")
+                nc.scalar.activation(out=scaled[:], in_=acc[t, 0][:], func=COPY, scale=one_minus_m[:, t : t + 1])
+                nc.gpsimd.tensor_tensor(out=result[:], in0=scaled[:], in1=parts[t][:], op=ADD)
+            else:
+                nc.vector.scalar_tensor_tensor(
+                    out=result[:], in0=acc[t, 0][:], scalar=one_minus_m[:, t : t + 1], in1=parts[t][:], op0=MULT, op1=ADD
+                )
+            for half in range(2):
+                nc.sync.dma_start(out=out_views[half][:, t, :], in_=result[:, half * FEAT : (half + 1) * FEAT])
+
+        def project(i):
+            tiles = range(i * GROUP, (i + 1) * GROUP)
+            if i == 0:
+                for t in tiles:
+                    reasoning_side(t)
+                for t in tiles:
+                    base_side(t)
+            else:
+                for t in tiles:
+                    reasoning_side(t)
+                    base_side(t)
+            if (i + 2) * GROUP - 1 < TILES - 1:
                 blend_biases_on_vector((i + 2) * GROUP - 1)
 
-        transpose_group(0)
+        transpose_tiles(range(2))
 
         nc.vector.tensor_scalar_mul(out=bias_rows[64:96, :], in0=bias_rows[64:96, :], scalar1=-1.0)
         nc.vector.tensor_copy(out=gate_by_tile[0:TILES, :], in_=gate_by_tile_bf[:])
@@ -234,10 +254,9 @@ def tile_reasoningmultiheadattention_pa_t_kernel(
         nc.vector.tensor_copy(out=m_f[:], in_=gate_ps[:, 0:TILES])
         one_minus_m = keep.tile([P, TILES], F32, name="one_minus_m")
         nc.vector.tensor_scalar(out=one_minus_m[:], in0=m_f[:], scalar1=-1.0, scalar2=1.0, op0=MULT, op1=ADD)
-
-        for t in range(GROUP):
+        for t in range(2):
             quantise(t)
-        transpose_group(1)
+
         spread = []
         for c in range(2):
             spread_ps = psum.tile([P, BANK], F32, name="spread_ps", tag="bank")
@@ -245,10 +264,19 @@ def tile_reasoningmultiheadattention_pa_t_kernel(
             spread.append(keep.tile([P, BANK], F32, name="spread%d" % c))
             nc.vector.tensor_copy(out=spread[c][:], in_=spread_ps[:])
         bias_base, bias_step = spread
+
+        transpose_tiles(range(2, GROUP))
+        blend_biases_on_vector(GROUP - 1)
+        for t in EARLY_BLENDS[0:3]:
+            blend_biases_on_vector(t)
+        for t in range(2, GROUP):
+            quantise(t)
+        transpose_tiles(range(GROUP, 2 * GROUP))
+        for t in EARLY_BLENDS[3:]:
+            blend_biases_on_vector(t)
         for t in range(GROUP - 1):
             blend_biases(t)
-        blend_biases_on_vector(GROUP - 1)
         for i in range(GROUPS):
             project(i)
             if i + 2 < GROUPS:
-                transpose_group(i + 2)
+                transpose_tiles(range((i + 2) * GROUP, (i + 3) * GROUP))

@@ -71,9 +71,9 @@ def tile_reasoningmultiheadattention_pa_t_kernel(
             cols = slice(half * FEAT, (half + 1) * FEAT)
             nc.scalar.dma_start(out=bias_rows[0:P:64, cols], in_=bias_in[0][half].unsqueeze(0).to_broadcast([2, FEAT]))
             nc.scalar.dma_start(out=bias_rows[32:33, cols], in_=bias_in[1][half].unsqueeze(0))
-        for queue, first, last in ((nc.scalar, 0, 2 * GROUP * P), (nc.gpsimd, 2 * GROUP * P, TOKENS)):
+        for first, last in ((0, 2 * GROUP * P), (2 * GROUP * P, TOKENS)):
             nc.vector.memset(gate_rows[:, first:last], 1.0)
-            queue.dma_start(
+            nc.gpsimd.dma_start(
                 out=gate_rows[32:65:32, first:last],
                 in_=gate_flat[first:last].unsqueeze(0).to_broadcast([2, last - first]),
             )
@@ -108,13 +108,12 @@ def tile_reasoningmultiheadattention_pa_t_kernel(
         scale_pieces = [(side, half, quad) for side in (1, 0) for half in range(2) for quad in range(4)]
         load_x(0, 0, 1)
         load_x(0, 1, 1)
-        load_scale_rows(scale_pieces[0:2])
         load_x(0, 2, 2)
-        load_scale_rows(scale_pieces[2:4])
+        load_scale_rows(scale_pieces[0:2])
         load_x(1, 0, 2)
-        load_scale_rows(scale_pieces[4:6])
+        load_scale_rows(scale_pieces[2:4])
         load_x(1, 2, 2)
-        load_scale_rows(scale_pieces[6:8])
+        load_scale_rows(scale_pieces[4:8])
         load_words(1)
         load_scale_rows(scale_pieces[8:12])
         load_words(0)
@@ -204,7 +203,7 @@ def tile_reasoningmultiheadattention_pa_t_kernel(
                 )
 
         def reasoning_side(t):
-            if t + 2 * GROUP < TILES:
+            if GROUP <= t < TILES - 2 * GROUP:
                 sort_words(t + 2 * GROUP)
             if t + BLENDS_AHEAD < TILES and not blended_by_vector(t + BLENDS_AHEAD):
                 blend_biases(t + BLENDS_AHEAD)
@@ -236,6 +235,7 @@ def tile_reasoningmultiheadattention_pa_t_kernel(
                 for t in tiles:
                     reasoning_side(t)
                 for t in tiles:
+                    sort_words(t + 2 * GROUP)
                     base_side(t)
             else:
                 for t in tiles:

@@ -51,7 +51,7 @@ def tile_reasoningmultiheadattention_pa_t_kernel(
         keep = ctx.enter_context(tc.tile_pool(name="keep", bufs=1))
         stage = ctx.enter_context(tc.tile_pool(name="stage", bufs=4))
         results = ctx.enter_context(tc.tile_pool(name="results", bufs=RESULTS_WAITING))
-        ahead = ctx.enter_context(tc.tile_pool(name="ahead", bufs=2 * GROUP))
+        ahead = ctx.enter_context(tc.tile_pool(name="ahead", bufs=GROUP))
         biases = ctx.enter_context(tc.tile_pool(name="biases", bufs=BLENDS_AHEAD + 2))
         sorted_pool = ctx.enter_context(tc.tile_pool(name="sorted_pool", bufs=2 * GROUP))
         psum = ctx.enter_context(tc.psum_pool(name="psum", bufs=8))
@@ -150,16 +150,21 @@ def tile_reasoningmultiheadattention_pa_t_kernel(
                             nc.tensor.transpose(
                                 xt[:, g, u, :], words[:, g * 256 + u : (g + 1) * 256 : 2], ident[:]
                             )
-                grouped[t] = ahead.tile([P, PASSES * P * 4], BF16, name="grouped", align_bytes=64)
+                if t % 2 == 0:
+                    grouped[t // 2] = ahead.tile([P, 2, PASSES * P * 4], BF16, name="grouped", align_bytes=64)
                 nc.scalar.copy(
-                    out=grouped[t][:].bitcast(F32).rearrange("p (g r u) -> p g r u", g=PASSES, u=2),
+                    out=grouped[t // 2][:, t % 2, :].bitcast(F32).rearrange("p (g r u) -> p g r u", g=PASSES, u=2),
                     in_=xt[:].rearrange("p g u r -> p g r u"),
                 )
 
-        def quantise(t):
-            codes[t] = ahead.tile([P, PASSES * P], U32, name="codes", align_bytes=64)
-            planes[t] = ahead.tile([P, PASSES * P], U8, name="planes", align_bytes=64)
-            nc.vector.quantize_mx(out=codes[t][:].bitcast(FP8X4), scales=planes[t][:], in_=grouped[t][:])
+        def quantise_pair(t):
+            codes[t // 2] = ahead.tile([P, 2 * PASSES * P], U32, name="codes", align_bytes=64)
+            planes[t // 2] = ahead.tile([P, 2 * PASSES * P], U8, name="planes", align_bytes=64)
+            nc.vector.quantize_mx(
+                out=codes[t // 2][:].bitcast(FP8X4),
+                scales=planes[t // 2][:],
+                in_=grouped[t // 2][:].rearrange("p j c -> p (j c)"),
+            )
 
         def blend_biases(t):
             blend_ps = psum.tile([P, BANK], F32, name="blend_ps", tag="bank")
@@ -192,10 +197,11 @@ def tile_reasoningmultiheadattention_pa_t_kernel(
             acc[t, side] = psum.tile([P, BANK], F32, name="acc%d" % side, tag="bank")
             for g in range(PASSES):
                 first = 8 * side + 4 * g
+                cols = slice(((t % 2) * PASSES + g) * P, ((t % 2) * PASSES + g + 1) * P)
                 nc.tensor.matmul_mx(
                     out=acc[t, side][:],
-                    lhsT=codes[t][:, g * P : (g + 1) * P].bitcast(FP8X4),
-                    lhsT_scale=planes[t][:, g * P : (g + 1) * P],
+                    lhsT=codes[t // 2][:, cols].bitcast(FP8X4),
+                    lhsT_scale=planes[t // 2][:, cols],
                     rhs=w_words[:, g, side, :].bitcast(FP8X4),
                     rhs_scale=w_planes[first:P, :],
                     start=(g == 0),
@@ -212,13 +218,15 @@ def tile_reasoningmultiheadattention_pa_t_kernel(
             nc.vector.scalar_tensor_tensor(
                 out=parts[t][:], in0=acc[t, 1][:], scalar=m_f[:, t : t + 1], in1=blended[t][:], op0=MULT, op1=ADD
             )
-            if t + GROUP < TILES:
-                quantise(t + GROUP)
+            if t % 2 == 0 and t + GROUP < TILES:
+                quantise_pair(t + GROUP)
+            if t % GROUP == 1 and t + GROUP + 2 < TILES - 1:
+                blend_biases_on_vector(t + GROUP + 2)
 
         def base_side(t):
             multiply(t, 0)
             result = results.tile([P, BANK], F32, name="result")
-            if t % GROUP == 1:
+            if t % GROUP == GROUP - 1 and t < TILES - 1:
                 scaled = stage.tile([P, BANK], F32, name="scaled")
                 nc.scalar.activation(out=scaled[:], in_=acc[t, 0][:], func=COPY, scale=one_minus_m[:, t : t + 1])
                 nc.gpsimd.tensor_tensor(out=result[:], in0=scaled[:], in1=parts[t][:], op=ADD)
@@ -241,8 +249,6 @@ def tile_reasoningmultiheadattention_pa_t_kernel(
                 for t in tiles:
                     reasoning_side(t)
                     base_side(t)
-            if (i + 2) * GROUP - 1 < TILES - 1:
-                blend_biases_on_vector((i + 2) * GROUP - 1)
 
         transpose_tiles(range(2))
 
@@ -254,8 +260,7 @@ def tile_reasoningmultiheadattention_pa_t_kernel(
         nc.vector.tensor_copy(out=m_f[:], in_=gate_ps[:, 0:TILES])
         one_minus_m = keep.tile([P, TILES], F32, name="one_minus_m")
         nc.vector.tensor_scalar(out=one_minus_m[:], in0=m_f[:], scalar1=-1.0, scalar2=1.0, op0=MULT, op1=ADD)
-        for t in range(2):
-            quantise(t)
+        quantise_pair(0)
 
         spread = []
         for c in range(2):
@@ -269,8 +274,7 @@ def tile_reasoningmultiheadattention_pa_t_kernel(
         blend_biases_on_vector(GROUP - 1)
         for t in EARLY_BLENDS[0:3]:
             blend_biases_on_vector(t)
-        for t in range(2, GROUP):
-            quantise(t)
+        quantise_pair(2)
         transpose_tiles(range(GROUP, 2 * GROUP))
         for t in EARLY_BLENDS[3:]:
             blend_biases_on_vector(t)

@@ -22,10 +22,15 @@ PASSES = HID // K_PASS
 BANK = 2 * FEAT
 TILES = TOKENS // P
 GROUP = 4
-GROUPS = TILES // GROUP
+RUNS = [range(0, 2), range(2, 4)] + [range(t, t + GROUP) for t in range(GROUP, TILES, GROUP)]
 RESULTS_WAITING = 16
-EARLY_BLENDS = range(GROUP + 2, TILES - GROUP, GROUP)
 BLENDS_AHEAD = 4
+
+ONES = 0x3F803F80
+
+BLEND_HEAD = "VVVVVVVV"
+BLEND_LOOP = "VPVV"
+G_ENDS = (1, 3)
 
 FLOPS = 2 * TOKENS * HID * 4 * FEAT
 
@@ -54,84 +59,83 @@ def tile_reasoningmultiheadattention_pa_t_kernel(
         ahead = ctx.enter_context(tc.tile_pool(name="ahead", bufs=GROUP))
         biases = ctx.enter_context(tc.tile_pool(name="biases", bufs=BLENDS_AHEAD + 2))
         sorted_pool = ctx.enter_context(tc.tile_pool(name="sorted_pool", bufs=2 * GROUP))
-        psum = ctx.enter_context(tc.psum_pool(name="psum", bufs=8))
+        psum = ctx.enter_context(tc.psum_pool(name="psum", bufs=7))
+        keep_psum = ctx.enter_context(tc.psum_pool(name="keep_psum", bufs=1))
 
+        w_planes = []
+        for side in range(2):
+            w_planes.append(keep.tile([P, BANK], U8, name="w_planes%d" % side, align_bytes=64))
+        nc.gpsimd.memset(w_planes[1][:].bitcast(I32), 0)
+        nc.vector.memset(w_planes[0][:].bitcast(I32), 0)
         ident = keep.tile([P, P], F32, name="ident")
         make_identity(nc, ident[:])
-        w_planes = keep.tile([P, BANK], U8, name="w_planes", align_bytes=64)
-        nc.vector.memset(w_planes[:].bitcast(I32), 0)
         bias_rows = keep.tile([P, BANK], BF16, name="bias_rows")
-        nc.vector.memset(bias_rows[:], 0.0)
+        nc.vector.memset(bias_rows[:].bitcast(I32), 0)
         gate_by_tile = keep.tile([P, P], F32, name="gate_by_tile")
         nc.vector.memset(gate_by_tile[:], 0.0)
-        gate_rows = keep.tile([P, TOKENS], BF16, name="gate_rows")
-        gate_by_tile_bf = keep.tile([TILES, P], BF16, name="gate_by_tile_bf")
-        nc.scalar.dma_start(out=gate_by_tile_bf[:], in_=gate_flat.rearrange("(t p) -> t p", p=P))
-        for half in range(2):
-            cols = slice(half * FEAT, (half + 1) * FEAT)
-            nc.scalar.dma_start(out=bias_rows[0:P:64, cols], in_=bias_in[0][half].unsqueeze(0).to_broadcast([2, FEAT]))
-            nc.scalar.dma_start(out=bias_rows[32:33, cols], in_=bias_in[1][half].unsqueeze(0))
-        for first, last in ((0, 2 * GROUP * P), (2 * GROUP * P, TOKENS)):
-            nc.vector.memset(gate_rows[:, first:last], 1.0)
-            nc.gpsimd.dma_start(
-                out=gate_rows[32:65:32, first:last],
-                in_=gate_flat[first:last].unsqueeze(0).to_broadcast([2, last - first]),
-            )
         pick = keep.tile([P, 2 * P], BF16, name="pick")
         nc.vector.memset(pick[:], 0.0)
         nc.vector.memset(pick[0:32, 0:P], 1.0)
         nc.vector.memset(pick[32:64, P : 2 * P], 1.0)
-        nc.vector.memset(pick[64:96, P : 2 * P], 1.0)
+        nc.vector.memset(pick[64:96, P : 2 * P], -1.0)
+        gate_rows = keep.tile([P, TOKENS], BF16, name="gate_rows")
 
-        x_sb = [keep.tile([P, GROUP, HID], BF16, name="x%d" % i) for i in range(GROUPS)]
+        x_sb = keep.tile([P, TILES, HID], BF16, name="x_sb")
         w_words = keep.tile([P, PASSES, 2, BANK], U32, name="w_words", align_bytes=64)
+        gate_by_tile_bf = keep.tile([TILES, P], BF16, name="gate_by_tile_bf")
 
-        def load_x(i, first, count):
-            t0 = i * GROUP + first
-            nc.sync.dma_start(out=x_sb[i][:, first : first + count, :], in_=x_view[:, t0 : t0 + count, :])
+        def load_x(queue, first, count):
+            queue.dma_start(out=x_sb[:, first : first + count, :], in_=x_view[:, first : first + count, :])
 
-        def load_scale_rows(pieces):
-            for side, half, quad in pieces:
-                first = 32 * quad + 8 * side
+        def load_scale_rows(side, half, quads):
+            for quad in quads:
                 nc.sync.dma_start(
-                    out=w_planes[first : first + 8, half * FEAT : (half + 1) * FEAT].bitcast(I32),
+                    out=w_planes[side][32 * quad : 32 * quad + 8, half * FEAT : (half + 1) * FEAT].bitcast(I32),
                     in_=scales_in[side][half][:, 4 * quad : 4 * quad + 4, :].bitcast(I32),
                 )
 
-        def load_words(side):
-            for half in range(2):
-                nc.sync.dma_start(
-                    out=w_words[:, :, side, half * FEAT : (half + 1) * FEAT].bitcast(I32),
-                    in_=words_in[side][half].rearrange("g p n t -> p g (n t)").bitcast(I32),
-                )
+        def load_words(side, half):
+            nc.sync.dma_start(
+                out=w_words[:, :, side, half * FEAT : (half + 1) * FEAT].bitcast(I32),
+                in_=words_in[side][half].rearrange("g p n t -> p g (n t)").bitcast(I32),
+            )
 
-        scale_pieces = [(side, half, quad) for side in (1, 0) for half in range(2) for quad in range(4)]
-        load_x(0, 0, 1)
-        load_x(0, 1, 1)
-        load_x(0, 2, 2)
-        load_scale_rows(scale_pieces[0:2])
-        load_x(1, 0, 2)
-        load_scale_rows(scale_pieces[2:4])
-        load_x(1, 2, 2)
-        load_scale_rows(scale_pieces[4:8])
-        load_words(1)
-        load_scale_rows(scale_pieces[8:12])
-        load_words(0)
-        load_scale_rows(scale_pieces[12:16])
-        load_x(2, 0, 2)
-        load_x(2, 2, 2)
-        for i in range(3, GROUPS):
-            load_x(i, 0, GROUP)
+        nc.gpsimd.dma_start(out=gate_by_tile_bf[:], in_=gate_flat.rearrange("(t p) -> t p", p=P))
+        for half in range(2):
+            cols = slice(half * FEAT, (half + 1) * FEAT)
+            nc.gpsimd.dma_start(out=bias_rows[0:P:64, cols], in_=bias_in[0][half].unsqueeze(0).to_broadcast([2, FEAT]))
+            nc.gpsimd.dma_start(out=bias_rows[32:33, cols], in_=bias_in[1][half].unsqueeze(0))
+        load_scale_rows(1, 0, range(4))
+        load_scale_rows(1, 1, range(2))
+        load_x(nc.scalar, 0, 2)
+        load_words(1, 0)
+        load_words(1, 1)
+        load_scale_rows(1, 1, range(2, 4))
+        load_x(nc.gpsimd, 2, 2)
+        warm = keep.tile([P, 1], F32, name="warm")
+        nc.vector.memset(warm[:], 0.0)
+        warm_out = keep.tile([P, 1], F32, name="warm_out")
+        nc.scalar.copy(out=warm_out[:], in_=warm[:])
+        load_scale_rows(0, 0, range(4))
+        load_scale_rows(0, 1, range(1))
+        load_words(0, 0)
+        load_words(0, 1)
+        load_scale_rows(0, 1, range(1, 4))
+        for t in range(4, 8, 2):
+            load_x(nc.sync, t, 2)
+        for t in range(8, TILES, GROUP):
+            load_x(nc.sync, t, GROUP)
+        nc.gpsimd.memset(gate_rows[:].bitcast(I32), ONES)
+        nc.gpsimd.dma_start(out=gate_rows[32:65:32, :], in_=gate_flat.unsqueeze(0).to_broadcast([2, TOKENS]))
 
         codes = {}
         planes = {}
         blended = {}
-
         grouped = {}
         sorted_words = {}
 
         def sort_words(t):
-            words = x_sb[t // GROUP][:, t % GROUP, :].bitcast(F32)
+            words = x_sb[:, t, :].bitcast(F32)
             sorted_words[t] = sorted_pool.tile([P, PASSES, 2, P], F32, name="sorted_words")
             nc.scalar.copy(
                 out=sorted_words[t][:], in_=words.rearrange("p (g r u) -> p g u r", g=PASSES, u=2)
@@ -139,14 +143,13 @@ def tile_reasoningmultiheadattention_pa_t_kernel(
 
         def transpose_tiles(tiles):
             for t in tiles:
-                i, j = divmod(t, GROUP)
                 xt = psum.tile([P, PASSES, 2, P], F32, name="xt", tag="bank")
                 for g in range(PASSES):
                     for u in range(2):
                         if t in sorted_words:
                             nc.tensor.transpose(xt[:, g, u, :], sorted_words[t][:, g, u, :], ident[:])
                         else:
-                            words = x_sb[i][:, j, :].bitcast(F32)
+                            words = x_sb[:, t, :].bitcast(F32)
                             nc.tensor.transpose(
                                 xt[:, g, u, :], words[:, g * 256 + u : (g + 1) * 256 : 2], ident[:]
                             )
@@ -166,29 +169,32 @@ def tile_reasoningmultiheadattention_pa_t_kernel(
                 in_=grouped[t // 2][:].rearrange("p j c -> p (j c)"),
             )
 
+        def blend_kind(t):
+            return BLEND_HEAD[t] if t < len(BLEND_HEAD) else BLEND_LOOP[t % GROUP]
+
         def blend_biases(t):
-            blend_ps = psum.tile([P, BANK], F32, name="blend_ps", tag="bank")
-            nc.tensor.matmul(
-                out=blend_ps[:],
-                lhsT=gate_rows[:, t * P : (t + 1) * P],
-                rhs=bias_rows[:],
-                start=True,
-                stop=True,
-            )
-            blended[t] = biases.tile([P, BANK], F32, name="blended")
-            nc.scalar.copy(out=blended[t][:], in_=blend_ps[:])
-
-        def blended_by_vector(t):
-            return (t % GROUP == GROUP - 1 and t < TILES - 1) or t in EARLY_BLENDS
-
-        def blend_biases_on_vector(t):
-            if t in EARLY_BLENDS:
-                blended[t] = keep.tile([P, BANK], F32, name="early%d" % t)
-            else:
+            kind = blend_kind(t)
+            if kind == "V":
                 blended[t] = biases.tile([P, BANK], F32, name="blended")
-            nc.vector.scalar_tensor_tensor(
-                out=blended[t][:], in0=bias_step[:], scalar=m_f[:, t : t + 1], in1=bias_base[:], op0=MULT, op1=ADD
-            )
+                nc.vector.scalar_tensor_tensor(
+                    out=blended[t][:], in0=bias_step[:], scalar=m_f[:, t : t + 1], in1=bias_base[:], op0=MULT, op1=ADD
+                )
+            elif kind == "G":
+                step = stage.tile([P, BANK], F32, name="step")
+                nc.scalar.activation(out=step[:], in_=bias_step[:], func=COPY, scale=m_f[:, t : t + 1])
+                blended[t] = biases.tile([P, BANK], F32, name="blended")
+                nc.gpsimd.tensor_tensor(out=blended[t][:], in0=step[:], in1=bias_base[:], op=ADD)
+            else:
+                blend_ps = psum.tile([P, BANK], F32, name="blend_ps", tag="bank")
+                nc.tensor.matmul(
+                    out=blend_ps[:],
+                    lhsT=gate_rows[:, t * P : (t + 1) * P],
+                    rhs=bias_rows[:],
+                    start=True,
+                    stop=True,
+                )
+                blended[t] = biases.tile([P, BANK], F32, name="blended")
+                nc.scalar.copy(out=blended[t][:], in_=blend_ps[:])
 
         acc = {}
         parts = {}
@@ -196,37 +202,28 @@ def tile_reasoningmultiheadattention_pa_t_kernel(
         def multiply(t, side):
             acc[t, side] = psum.tile([P, BANK], F32, name="acc%d" % side, tag="bank")
             for g in range(PASSES):
-                first = 8 * side + 4 * g
                 cols = slice(((t % 2) * PASSES + g) * P, ((t % 2) * PASSES + g + 1) * P)
                 nc.tensor.matmul_mx(
                     out=acc[t, side][:],
                     lhsT=codes[t // 2][:, cols].bitcast(FP8X4),
                     lhsT_scale=planes[t // 2][:, cols],
                     rhs=w_words[:, g, side, :].bitcast(FP8X4),
-                    rhs_scale=w_planes[first:P, :],
+                    rhs_scale=w_planes[side][4 * g : P, :],
                     start=(g == 0),
                     stop=(g == PASSES - 1),
                 )
 
         def reasoning_side(t):
-            if GROUP <= t < TILES - 2 * GROUP:
-                sort_words(t + 2 * GROUP)
-            if t + BLENDS_AHEAD < TILES and not blended_by_vector(t + BLENDS_AHEAD):
-                blend_biases(t + BLENDS_AHEAD)
             multiply(t, 1)
             parts[t] = stage.tile([P, BANK], F32, name="part")
             nc.vector.scalar_tensor_tensor(
                 out=parts[t][:], in0=acc[t, 1][:], scalar=m_f[:, t : t + 1], in1=blended[t][:], op0=MULT, op1=ADD
             )
-            if t % 2 == 0 and t + GROUP < TILES:
-                quantise_pair(t + GROUP)
-            if t % GROUP == 1 and t + GROUP + 2 < TILES - 1:
-                blend_biases_on_vector(t + GROUP + 2)
 
         def base_side(t):
             multiply(t, 0)
             result = results.tile([P, BANK], F32, name="result")
-            if t % GROUP == GROUP - 1 and t < TILES - 1:
+            if t % GROUP in G_ENDS and t < TILES - 2:
                 scaled = stage.tile([P, BANK], F32, name="scaled")
                 nc.scalar.activation(out=scaled[:], in_=acc[t, 0][:], func=COPY, scale=one_minus_m[:, t : t + 1])
                 nc.gpsimd.tensor_tensor(out=result[:], in0=scaled[:], in1=parts[t][:], op=ADD)
@@ -237,22 +234,25 @@ def tile_reasoningmultiheadattention_pa_t_kernel(
             for half in range(2):
                 nc.sync.dma_start(out=out_views[half][:, t, :], in_=result[:, half * FEAT : (half + 1) * FEAT])
 
-        def project(i):
-            tiles = range(i * GROUP, (i + 1) * GROUP)
-            if i == 0:
-                for t in tiles:
-                    reasoning_side(t)
-                for t in tiles:
-                    sort_words(t + 2 * GROUP)
-                    base_side(t)
-            else:
-                for t in tiles:
-                    reasoning_side(t)
-                    base_side(t)
+        def pair(t):
+            for j in (t, t + 1):
+                if j + BLENDS_AHEAD < TILES and blend_kind(j + BLENDS_AHEAD) == "P":
+                    blend_biases(j + BLENDS_AHEAD)
+            for j in (t, t + 1):
+                reasoning_side(j)
+            if t == 0:
+                transpose_tiles(RUNS[1])
+                blend_biases(2)
+                blend_biases(3)
+                quantise_pair(2)
+            elif t + GROUP < TILES:
+                quantise_pair(t + GROUP)
+            for j in (t, t + 1):
+                base_side(j)
+            for j in (t, t + 1):
+                if j + BLENDS_AHEAD < TILES and blend_kind(j + BLENDS_AHEAD) != "P":
+                    blend_biases(j + BLENDS_AHEAD)
 
-        transpose_tiles(range(2))
-
-        nc.vector.tensor_scalar_mul(out=bias_rows[64:96, :], in0=bias_rows[64:96, :], scalar1=-1.0)
         nc.vector.tensor_copy(out=gate_by_tile[0:TILES, :], in_=gate_by_tile_bf[:])
         gate_ps = psum.tile([P, P], F32, name="gate_ps", tag="bank")
         nc.tensor.transpose(gate_ps[:], gate_by_tile[:], ident[:])
@@ -260,27 +260,26 @@ def tile_reasoningmultiheadattention_pa_t_kernel(
         nc.vector.tensor_copy(out=m_f[:], in_=gate_ps[:, 0:TILES])
         one_minus_m = keep.tile([P, TILES], F32, name="one_minus_m")
         nc.vector.tensor_scalar(out=one_minus_m[:], in0=m_f[:], scalar1=-1.0, scalar2=1.0, op0=MULT, op1=ADD)
+
+        transpose_tiles(RUNS[0])
+        base_ps = psum.tile([P, BANK], F32, name="base_ps", tag="bank")
+        nc.tensor.matmul(out=base_ps[:], lhsT=pick[:, 0:P], rhs=bias_rows[:], start=True, stop=True)
+        bias_base = keep.tile([P, BANK], F32, name="bias_base")
+        nc.scalar.copy(out=bias_base[:], in_=base_ps[:])
+        bias_step = keep_psum.tile([P, BANK], F32, name="bias_step")
+        nc.tensor.matmul(out=bias_step[:], lhsT=pick[:, P : 2 * P], rhs=bias_rows[:], start=True, stop=True)
+
         quantise_pair(0)
-
-        spread = []
-        for c in range(2):
-            spread_ps = psum.tile([P, BANK], F32, name="spread_ps", tag="bank")
-            nc.tensor.matmul(out=spread_ps[:], lhsT=pick[:, c * P : (c + 1) * P], rhs=bias_rows[:], start=True, stop=True)
-            spread.append(keep.tile([P, BANK], F32, name="spread%d" % c))
-            nc.vector.tensor_copy(out=spread[c][:], in_=spread_ps[:])
-        bias_base, bias_step = spread
-
-        transpose_tiles(range(2, GROUP))
-        blend_biases_on_vector(GROUP - 1)
-        for t in EARLY_BLENDS[0:3]:
-            blend_biases_on_vector(t)
-        quantise_pair(2)
-        transpose_tiles(range(GROUP, 2 * GROUP))
-        for t in EARLY_BLENDS[3:]:
-            blend_biases_on_vector(t)
-        for t in range(GROUP - 1):
-            blend_biases(t)
-        for i in range(GROUPS):
-            project(i)
-            if i + 2 < GROUPS:
-                transpose_tiles(range((i + 2) * GROUP, (i + 3) * GROUP))
+        blend_biases(0)
+        blend_biases(1)
+        nc.vector.tensor_scalar_mul(out=bias_rows[64:96, :], in0=bias_rows[64:96, :], scalar1=-1.0)
+        for i, tiles in enumerate(RUNS):
+            for t in tiles:
+                if GROUP <= t and t + 2 * GROUP < TILES:
+                    sort_words(t + 2 * GROUP)
+                if t % 2 == 1:
+                    pair(t - 1)
+            if i + 2 < len(RUNS):
+                transpose_tiles(RUNS[i + 2])
+                if i == 0:
+                    quantise_pair(4)

@@ -65,12 +65,10 @@ def tile_reasoningmultiheadattention_pa_t_kernel(
         w_planes = []
         for side in range(2):
             w_planes.append(keep.tile([P, BANK], U8, name="w_planes%d" % side, align_bytes=64))
-        nc.gpsimd.memset(w_planes[1][:].bitcast(I32), 0)
-        nc.vector.memset(w_planes[0][:].bitcast(I32), 0)
-        ident = keep.tile([P, P], F32, name="ident")
-        make_identity(nc, ident[:])
+        nc.vector.memset(w_planes[1][:].bitcast(I32), 0)
         bias_rows = keep.tile([P, BANK], BF16, name="bias_rows")
-        nc.vector.memset(bias_rows[:].bitcast(I32), 0)
+        nc.gpsimd.memset(bias_rows[:].bitcast(I32), 0)
+        nc.vector.memset(w_planes[0][:].bitcast(I32), 0)
         gate_by_tile = keep.tile([P, P], F32, name="gate_by_tile")
         nc.vector.memset(gate_by_tile[:], 0.0)
         pick = keep.tile([P, 2 * P], BF16, name="pick")
@@ -100,27 +98,31 @@ def tile_reasoningmultiheadattention_pa_t_kernel(
                 in_=words_in[side][half].rearrange("g p n t -> p g (n t)").bitcast(I32),
             )
 
-        nc.gpsimd.dma_start(out=gate_by_tile_bf[:], in_=gate_flat.rearrange("(t p) -> t p", p=P))
-        for half in range(2):
+        def load_biases(half):
             cols = slice(half * FEAT, (half + 1) * FEAT)
             nc.gpsimd.dma_start(out=bias_rows[0:P:64, cols], in_=bias_in[0][half].unsqueeze(0).to_broadcast([2, FEAT]))
             nc.gpsimd.dma_start(out=bias_rows[32:33, cols], in_=bias_in[1][half].unsqueeze(0))
+
+        load_biases(0)
+        ident = keep.tile([P, P], F32, name="ident")
+        make_identity(nc, ident[:])
+        load_biases(1)
         load_scale_rows(1, 0, range(4))
-        load_scale_rows(1, 1, range(2))
         load_x(nc.scalar, 0, 2)
-        load_words(1, 0)
-        load_words(1, 1)
-        load_scale_rows(1, 1, range(2, 4))
-        load_x(nc.gpsimd, 2, 2)
+        nc.scalar.dma_start(out=gate_by_tile_bf[:], in_=gate_flat.rearrange("(t p) -> t p", p=P))
         warm = keep.tile([P, 1], F32, name="warm")
         nc.vector.memset(warm[:], 0.0)
         warm_out = keep.tile([P, 1], F32, name="warm_out")
         nc.scalar.copy(out=warm_out[:], in_=warm[:])
-        load_scale_rows(0, 0, range(4))
-        load_scale_rows(0, 1, range(1))
+        load_words(1, 0)
+        load_words(1, 1)
+        load_scale_rows(1, 1, range(4))
+        load_x(nc.sync, 2, 2)
         load_words(0, 0)
+        load_scale_rows(0, 0, range(2))
         load_words(0, 1)
-        load_scale_rows(0, 1, range(1, 4))
+        load_scale_rows(0, 0, range(2, 4))
+        load_scale_rows(0, 1, range(4))
         for t in range(4, 8, 2):
             load_x(nc.sync, t, 2)
         for t in range(8, TILES, GROUP):
@@ -240,12 +242,7 @@ def tile_reasoningmultiheadattention_pa_t_kernel(
                     blend_biases(j + BLENDS_AHEAD)
             for j in (t, t + 1):
                 reasoning_side(j)
-            if t == 0:
-                transpose_tiles(RUNS[1])
-                blend_biases(2)
-                blend_biases(3)
-                quantise_pair(2)
-            elif t + GROUP < TILES:
+            if t + GROUP < TILES:
                 quantise_pair(t + GROUP)
             for j in (t, t + 1):
                 base_side(j)
@@ -273,7 +270,29 @@ def tile_reasoningmultiheadattention_pa_t_kernel(
         blend_biases(0)
         blend_biases(1)
         nc.vector.tensor_scalar_mul(out=bias_rows[64:96, :], in0=bias_rows[64:96, :], scalar1=-1.0)
+        for t in range(2):
+            reasoning_side(t)
+        transpose_tiles(RUNS[1])
+        quantise_pair(2)
+        blend_biases(2)
+        blend_biases(3)
+        for t in range(2, 4):
+            reasoning_side(t)
+        for t in range(2):
+            base_side(t)
+            blend_biases(t + 4)
+        transpose_tiles(range(4, 6))
+        for t in range(2, 4):
+            base_side(t)
+        quantise_pair(4)
+        transpose_tiles(range(6, 8))
+        for t in range(2, 4):
+            blend_biases(t + 4)
+        quantise_pair(6)
+        transpose_tiles(RUNS[3])
         for i, tiles in enumerate(RUNS):
+            if i < 2:
+                continue
             for t in tiles:
                 if GROUP <= t and t + 2 * GROUP < TILES:
                     sort_words(t + 2 * GROUP)
@@ -281,5 +300,3 @@ def tile_reasoningmultiheadattention_pa_t_kernel(
                     pair(t - 1)
             if i + 2 < len(RUNS):
                 transpose_tiles(RUNS[i + 2])
-                if i == 0:
-                    quantise_pair(4)

@@ -28,7 +28,7 @@ BLENDS_AHEAD = 4
 
 ONES = 0x3F803F80
 
-BLEND_HEAD = "VVVVVVVV"
+BLEND_HEAD = "VVGGGGGG"
 BLEND_LOOP = "VPVV"
 G_ENDS = (1, 3)
 
@@ -67,7 +67,7 @@ def tile_reasoningmultiheadattention_pa_t_kernel(
             w_planes.append(keep.tile([P, BANK], U8, name="w_planes%d" % side, align_bytes=64))
         nc.vector.memset(w_planes[1][:].bitcast(I32), 0)
         bias_rows = keep.tile([P, BANK], BF16, name="bias_rows")
-        nc.gpsimd.memset(bias_rows[:].bitcast(I32), 0)
+        nc.vector.memset(bias_rows[:].bitcast(I32), 0)
         nc.vector.memset(w_planes[0][:].bitcast(I32), 0)
         gate_by_tile = keep.tile([P, P], F32, name="gate_by_tile")
         nc.vector.memset(gate_by_tile[:], 0.0)
@@ -98,28 +98,34 @@ def tile_reasoningmultiheadattention_pa_t_kernel(
                 in_=words_in[side][half].rearrange("g p n t -> p g (n t)").bitcast(I32),
             )
 
-        def load_biases(half):
+        def load_biases(queue, side, half):
             cols = slice(half * FEAT, (half + 1) * FEAT)
-            nc.gpsimd.dma_start(out=bias_rows[0:P:64, cols], in_=bias_in[0][half].unsqueeze(0).to_broadcast([2, FEAT]))
-            nc.gpsimd.dma_start(out=bias_rows[32:33, cols], in_=bias_in[1][half].unsqueeze(0))
+            row = bias_in[side][half].unsqueeze(0)
+            if side == 0:
+                queue.dma_start(out=bias_rows[0:P:64, cols], in_=row.to_broadcast([2, FEAT]))
+            else:
+                queue.dma_start(out=bias_rows[32:33, cols], in_=row)
 
-        load_biases(0)
+        nc.gpsimd.dma_start(out=gate_by_tile_bf[:], in_=gate_flat.rearrange("(t p) -> t p", p=P))
         ident = keep.tile([P, P], F32, name="ident")
         make_identity(nc, ident[:])
-        load_biases(1)
+        load_biases(nc.gpsimd, 0, 0)
+        load_x(nc.gpsimd, 2, 2)
         load_scale_rows(1, 0, range(4))
+        load_scale_rows(1, 1, range(3))
         load_x(nc.scalar, 0, 2)
-        nc.scalar.dma_start(out=gate_by_tile_bf[:], in_=gate_flat.rearrange("(t p) -> t p", p=P))
         warm = keep.tile([P, 1], F32, name="warm")
         nc.vector.memset(warm[:], 0.0)
         warm_out = keep.tile([P, 1], F32, name="warm_out")
         nc.scalar.copy(out=warm_out[:], in_=warm[:])
         load_words(1, 0)
         load_words(1, 1)
-        load_scale_rows(1, 1, range(4))
-        load_x(nc.sync, 2, 2)
-        load_words(0, 0)
+        load_biases(nc.sync, 0, 1)
+        load_biases(nc.sync, 1, 0)
+        load_biases(nc.sync, 1, 1)
+        load_scale_rows(1, 1, range(3, 4))
         load_scale_rows(0, 0, range(2))
+        load_words(0, 0)
         load_words(0, 1)
         load_scale_rows(0, 0, range(2, 4))
         load_scale_rows(0, 1, range(4))
@@ -242,7 +248,9 @@ def tile_reasoningmultiheadattention_pa_t_kernel(
                     blend_biases(j + BLENDS_AHEAD)
             for j in (t, t + 1):
                 reasoning_side(j)
-            if t + GROUP < TILES:
+            if t == GROUP + 2:
+                quantise_pair(t + 2)
+            if t > GROUP and t + GROUP < TILES:
                 quantise_pair(t + GROUP)
             for j in (t, t + 1):
                 base_side(j)
@@ -250,6 +258,7 @@ def tile_reasoningmultiheadattention_pa_t_kernel(
                 if j + BLENDS_AHEAD < TILES and blend_kind(j + BLENDS_AHEAD) != "P":
                     blend_biases(j + BLENDS_AHEAD)
 
+        transpose_tiles(RUNS[0])
         nc.vector.tensor_copy(out=gate_by_tile[0:TILES, :], in_=gate_by_tile_bf[:])
         gate_ps = psum.tile([P, P], F32, name="gate_ps", tag="bank")
         nc.tensor.transpose(gate_ps[:], gate_by_tile[:], ident[:])
@@ -258,7 +267,6 @@ def tile_reasoningmultiheadattention_pa_t_kernel(
         one_minus_m = keep.tile([P, TILES], F32, name="one_minus_m")
         nc.vector.tensor_scalar(out=one_minus_m[:], in0=m_f[:], scalar1=-1.0, scalar2=1.0, op0=MULT, op1=ADD)
 
-        transpose_tiles(RUNS[0])
         base_ps = psum.tile([P, BANK], F32, name="base_ps", tag="bank")
         nc.tensor.matmul(out=base_ps[:], lhsT=pick[:, 0:P], rhs=bias_rows[:], start=True, stop=True)
         bias_base = keep.tile([P, BANK], F32, name="bias_base")
@@ -272,15 +280,15 @@ def tile_reasoningmultiheadattention_pa_t_kernel(
         nc.vector.tensor_scalar_mul(out=bias_rows[64:96, :], in0=bias_rows[64:96, :], scalar1=-1.0)
         for t in range(2):
             reasoning_side(t)
-        transpose_tiles(RUNS[1])
-        quantise_pair(2)
         blend_biases(2)
         blend_biases(3)
-        for t in range(2, 4):
-            reasoning_side(t)
+        transpose_tiles(RUNS[1])
+        quantise_pair(2)
         for t in range(2):
             base_side(t)
             blend_biases(t + 4)
+        for t in range(2, 4):
+            reasoning_side(t)
         transpose_tiles(range(4, 6))
         for t in range(2, 4):
             base_side(t)
@@ -289,14 +297,15 @@ def tile_reasoningmultiheadattention_pa_t_kernel(
         for t in range(2, 4):
             blend_biases(t + 4)
         quantise_pair(6)
-        transpose_tiles(RUNS[3])
         for i, tiles in enumerate(RUNS):
             if i < 2:
                 continue
             for t in tiles:
-                if GROUP <= t and t + 2 * GROUP < TILES:
+                if t + 2 * GROUP < TILES:
                     sort_words(t + 2 * GROUP)
                 if t % 2 == 1:
                     pair(t - 1)
+                if t == 5:
+                    transpose_tiles(RUNS[3])
             if i + 2 < len(RUNS):
                 transpose_tiles(RUNS[i + 2])

@@ -28,9 +28,12 @@ BLENDS_AHEAD = 4
 
 ONES = 0x3F803F80
 
-BLEND_HEAD = "VVGGGGGG"
-BLEND_LOOP = "VPVV"
-G_ENDS = (1, 3)
+BLEND_HEAD = "VVVVVVVV"
+BLEND_TAIL = "PPPP"
+TAIL = 28
+BLEND_LOOP = "VPVP"
+G_FROM = 4
+G_ENDS = (3,)
 
 FLOPS = 2 * TOKENS * HID * 4 * FEAT
 
@@ -178,7 +181,9 @@ def tile_reasoningmultiheadattention_pa_t_kernel(
             )
 
         def blend_kind(t):
-            return BLEND_HEAD[t] if t < len(BLEND_HEAD) else BLEND_LOOP[t % GROUP]
+            if t < len(BLEND_HEAD):
+                return BLEND_HEAD[t]
+            return BLEND_TAIL[t % GROUP] if t >= TAIL else BLEND_LOOP[t % GROUP]
 
         def blend_biases(t):
             kind = blend_kind(t)
@@ -231,7 +236,7 @@ def tile_reasoningmultiheadattention_pa_t_kernel(
         def base_side(t):
             multiply(t, 0)
             result = results.tile([P, BANK], F32, name="result")
-            if t % GROUP in G_ENDS and t < TILES - 2:
+            if t % GROUP in G_ENDS and G_FROM <= t < TILES - 2:
                 scaled = stage.tile([P, BANK], F32, name="scaled")
                 nc.scalar.activation(out=scaled[:], in_=acc[t, 0][:], func=COPY, scale=one_minus_m[:, t : t + 1])
                 nc.gpsimd.tensor_tensor(out=result[:], in0=scaled[:], in1=parts[t][:], op=ADD)
@@ -277,13 +282,13 @@ def tile_reasoningmultiheadattention_pa_t_kernel(
         quantise_pair(0)
         blend_biases(0)
         blend_biases(1)
-        nc.vector.tensor_scalar_mul(out=bias_rows[64:96, :], in0=bias_rows[64:96, :], scalar1=-1.0)
         for t in range(2):
             reasoning_side(t)
+        transpose_tiles(RUNS[1])
+        nc.scalar.activation(out=bias_rows[64:96, :], in_=bias_rows[64:96, :], func=COPY, scale=-1.0)
+        quantise_pair(2)
         blend_biases(2)
         blend_biases(3)
-        transpose_tiles(RUNS[1])
-        quantise_pair(2)
         for t in range(2):
             base_side(t)
             blend_biases(t + 4)

@@ -30,10 +30,13 @@ ONES = 0x3F803F80
 
 BLEND_HEAD = "VVVVVVVV"
 BLEND_TAIL = "PPPP"
+QLEAD = 4
+TLEAD = 6
+SLEAD = 8
 TAIL = 28
-BLEND_LOOP = "VPVP"
+BLEND_LOOP = "VPVV"
 G_FROM = 4
-G_ENDS = (3,)
+G_ENDS = (1, 3)
 
 FLOPS = 2 * TOKENS * HID * 4 * FEAT
 
@@ -134,7 +137,9 @@ def tile_reasoningmultiheadattention_pa_t_kernel(
         load_scale_rows(0, 1, range(4))
         for t in range(4, 8, 2):
             load_x(nc.sync, t, 2)
-        for t in range(8, TILES, GROUP):
+        for t in range(8, 12, 2):
+            load_x(nc.sync, t, 2)
+        for t in range(12, TILES, GROUP):
             load_x(nc.sync, t, GROUP)
         nc.gpsimd.memset(gate_rows[:].bitcast(I32), ONES)
         nc.gpsimd.dma_start(out=gate_rows[32:65:32, :], in_=gate_flat.unsqueeze(0).to_broadcast([2, TOKENS]))
@@ -253,10 +258,8 @@ def tile_reasoningmultiheadattention_pa_t_kernel(
                     blend_biases(j + BLENDS_AHEAD)
             for j in (t, t + 1):
                 reasoning_side(j)
-            if t == GROUP + 2:
-                quantise_pair(t + 2)
-            if t > GROUP and t + GROUP < TILES:
-                quantise_pair(t + GROUP)
+            if t + QLEAD < TILES:
+                quantise_pair(t + QLEAD)
             for j in (t, t + 1):
                 base_side(j)
             for j in (t, t + 1):
@@ -302,15 +305,11 @@ def tile_reasoningmultiheadattention_pa_t_kernel(
         for t in range(2, 4):
             blend_biases(t + 4)
         quantise_pair(6)
-        for i, tiles in enumerate(RUNS):
-            if i < 2:
-                continue
-            for t in tiles:
-                if t + 2 * GROUP < TILES:
-                    sort_words(t + 2 * GROUP)
-                if t % 2 == 1:
-                    pair(t - 1)
-                if t == 5:
-                    transpose_tiles(RUNS[3])
-            if i + 2 < len(RUNS):
-                transpose_tiles(RUNS[i + 2])
+        transpose_tiles(range(8, 10))
+        for t in range(GROUP, TILES, 2):
+            for j in (t, t + 1):
+                if j + SLEAD < TILES:
+                    sort_words(j + SLEAD)
+            pair(t)
+            if t + TLEAD < TILES:
+                transpose_tiles(range(t + TLEAD, t + TLEAD + 2))

@@ -70,7 +70,7 @@ def tile_reasoningmultiheadattention_pa_t_kernel(
 
         w_planes = []
         for side in range(2):
-            w_planes.append(keep.tile([P, BANK], U8, name="w_planes%d" % side, align_bytes=64))
+            w_planes.append(keep.tile([P, BANK], U8, name="w_planes%d" % side, align_bytes=256))
         nc.vector.memset(w_planes[1][:].bitcast(I32), 0)
         bias_rows = keep.tile([P, BANK], BF16, name="bias_rows")
         nc.vector.memset(bias_rows[:].bitcast(I32), 0)
@@ -85,7 +85,7 @@ def tile_reasoningmultiheadattention_pa_t_kernel(
         gate_rows = keep.tile([P, TOKENS], BF16, name="gate_rows")
 
         x_sb = keep.tile([P, TILES, HID], BF16, name="x_sb")
-        w_words = keep.tile([P, PASSES, 2, BANK], U32, name="w_words", align_bytes=64)
+        w_words = keep.tile([P, PASSES, 2, BANK], U32, name="w_words", align_bytes=256)
         gate_by_tile_bf = keep.tile([TILES, P], BF16, name="gate_by_tile_bf")
 
         def load_x(queue, first, count):
@@ -170,15 +170,15 @@ def tile_reasoningmultiheadattention_pa_t_kernel(
                                 xt[:, g, u, :], words[:, g * 256 + u : (g + 1) * 256 : 2], ident[:]
                             )
                 if t % 2 == 0:
-                    grouped[t // 2] = ahead.tile([P, 2, PASSES * P * 4], BF16, name="grouped", align_bytes=64)
+                    grouped[t // 2] = ahead.tile([P, 2, PASSES * P * 4], BF16, name="grouped", align_bytes=256)
                 nc.scalar.copy(
                     out=grouped[t // 2][:, t % 2, :].bitcast(F32).rearrange("p (g r u) -> p g r u", g=PASSES, u=2),
                     in_=xt[:].rearrange("p g u r -> p g r u"),
                 )
 
         def quantise_pair(t):
-            codes[t // 2] = ahead.tile([P, 2 * PASSES * P], U32, name="codes", align_bytes=64)
-            planes[t // 2] = ahead.tile([P, 2 * PASSES * P], U8, name="planes", align_bytes=64)
+            codes[t // 2] = ahead.tile([P, 2 * PASSES * P], U32, name="codes", align_bytes=256)
+            planes[t // 2] = ahead.tile([P, 2 * PASSES * P], U8, name="planes", align_bytes=256)
             nc.vector.quantize_mx(
                 out=codes[t // 2][:].bitcast(FP8X4),
                 scales=planes[t // 2][:],
@@ -244,7 +244,9 @@ def tile_reasoningmultiheadattention_pa_t_kernel(
             if t % GROUP in G_ENDS and G_FROM <= t < TILES - 2:
                 scaled = stage.tile([P, BANK], F32, name="scaled")
                 nc.scalar.activation(out=scaled[:], in_=acc[t, 0][:], func=COPY, scale=one_minus_m[:, t : t + 1])
-                nc.gpsimd.tensor_tensor(out=result[:], in0=scaled[:], in1=parts[t][:], op=ADD)
+                for half in range(2):
+                    cols = slice(half * FEAT, (half + 1) * FEAT)
+                    nc.gpsimd.tensor_tensor(out=result[:, cols], in0=scaled[:, cols], in1=parts[t][:, cols], op=ADD)
             else:
                 nc.vector.scalar_tensor_tensor(
                     out=result[:], in0=acc[t, 0][:], scalar=one_minus_m[:, t : t + 1], in1=parts[t][:], op0=MULT, op1=ADD

from contextlib import ExitStack

import concourse.mybir as mybir
from concourse.masks import make_identity

F32 = mybir.dt.float32
BF16 = mybir.dt.bfloat16
I32 = mybir.dt.int32
U32 = mybir.dt.uint32
U8 = mybir.dt.uint8
FP8X4 = mybir.dt.float8_e4m3fn_x4
MULT = mybir.AluOpType.mult
ADD = mybir.AluOpType.add
COPY = mybir.ActivationFunctionType.Copy

P = 128
TOKENS = 4096
HID = 1024
FEAT = 256
K_PASS = 512
PASSES = HID // K_PASS
BANK = 2 * FEAT
TILES = TOKENS // P
GROUP = 4
RUNS = [range(0, 2), range(2, 4)] + [range(t, t + GROUP) for t in range(GROUP, TILES, GROUP)]
RESULTS_WAITING = 16
BLENDS_AHEAD = 4

ONES = 0x3F803F80

BLEND_HEAD = "VVVVVVVV"
BLEND_TAIL = "PPPP"
QLEAD = 4
TLEAD = 6
SLEAD = 8
TAIL = 28
BLEND_LOOP = "VPVV"
G_FROM = 4
G_ENDS = (1, 3)

FLOPS = 2 * TOKENS * HID * 4 * FEAT


def tile_reasoningmultiheadattention_pa_t_kernel(
    tc, x, reasoning_mask,
    Wq_words, Wq_scales, bq, Wk_words, Wk_scales, bk,
    Wqr_words, Wqr_scales, bqr, Wkr_words, Wkr_scales, bkr,
    out_0, out_1,
):
    nc = tc.nc
    x_view = x.rearrange("b s k -> (b s) k").rearrange("(t p) k -> p t k", p=P)
    gate_flat = reasoning_mask.rearrange("b s o i -> (b s o i)")
    out_views = [
        o.rearrange("b s h d -> (b s) (h d)").rearrange("(t p) n -> p t n", p=P) for o in (out_0, out_1)
    ]
    words_in = [[Wq_words, Wk_words], [Wqr_words, Wkr_words]]
    scales_in = [[Wq_scales, Wk_scales], [Wqr_scales, Wkr_scales]]
    bias_in = [[bq, bk], [bqr, bkr]]

    with ExitStack() as ctx:
        ctx.enter_context(tc.manual_schedule())
        keep = ctx.enter_context(tc.tile_pool(name="keep", bufs=1))
        stage = ctx.enter_context(tc.tile_pool(name="stage", bufs=4))
        results = ctx.enter_context(tc.tile_pool(name="results", bufs=RESULTS_WAITING))
        ahead = ctx.enter_context(tc.tile_pool(name="ahead", bufs=GROUP))
        biases = ctx.enter_context(tc.tile_pool(name="biases", bufs=BLENDS_AHEAD + 2))
        sorted_pool = ctx.enter_context(tc.tile_pool(name="sorted_pool", bufs=2 * GROUP))
        psum = ctx.enter_context(tc.psum_pool(name="psum", bufs=7))
        keep_psum = ctx.enter_context(tc.psum_pool(name="keep_psum", bufs=1))

        w_planes = []
        for side in range(2):
            w_planes.append(keep.tile([P, BANK], U8, name="w_planes%d" % side, align_bytes=256))
        nc.vector.memset(w_planes[1][:].bitcast(I32), 0)
        bias_rows = keep.tile([P, BANK], BF16, name="bias_rows")
        nc.vector.memset(bias_rows[:].bitcast(I32), 0)
        nc.vector.memset(w_planes[0][:].bitcast(I32), 0)
        gate_by_tile = keep.tile([P, P], F32, name="gate_by_tile")
        nc.vector.memset(gate_by_tile[:], 0.0)
        pick = keep.tile([P, 2 * P], BF16, name="pick")
        nc.vector.memset(pick[:], 0.0)
        nc.vector.memset(pick[0:32, 0:P], 1.0)
        nc.vector.memset(pick[32:64, P : 2 * P], 1.0)
        nc.vector.memset(pick[64:96, P : 2 * P], -1.0)
        gate_rows = keep.tile([P, TOKENS], BF16, name="gate_rows")

        x_sb = keep.tile([P, TILES, HID], BF16, name="x_sb")
        w_words = keep.tile([P, PASSES, 2, BANK], U32, name="w_words", align_bytes=256)
        gate_by_tile_bf = keep.tile([TILES, P], BF16, name="gate_by_tile_bf")

        def load_x(queue, first, count):
            queue.dma_start(out=x_sb[:, first : first + count, :], in_=x_view[:, first : first + count, :])

        def load_scale_rows(side, half, quads):
            for quad in quads:
                nc.sync.dma_start(
                    out=w_planes[side][32 * quad : 32 * quad + 8, half * FEAT : (half + 1) * FEAT].bitcast(I32),
                    in_=scales_in[side][half][:, 4 * quad : 4 * quad + 4, :].bitcast(I32),
                )

        def load_words(side, half):
            nc.sync.dma_start(
                out=w_words[:, :, side, half * FEAT : (half + 1) * FEAT].bitcast(I32),
                in_=words_in[side][half].rearrange("g p n t -> p g (n t)").bitcast(I32),
            )

        def load_biases(queue, side, half):
            cols = slice(half * FEAT, (half + 1) * FEAT)
            row = bias_in[side][half].unsqueeze(0)
            if side == 0:
                queue.dma_start(out=bias_rows[0:P:64, cols], in_=row.to_broadcast([2, FEAT]))
            else:
                queue.dma_start(out=bias_rows[32:33, cols], in_=row)

        nc.gpsimd.dma_start(out=gate_by_tile_bf[:], in_=gate_flat.rearrange("(t p) -> t p", p=P))
        ident = keep.tile([P, P], F32, name="ident")
        make_identity(nc, ident[:])
        load_biases(nc.gpsimd, 0, 0)
        load_x(nc.gpsimd, 2, 2)
        load_scale_rows(1, 0, range(4))
        load_scale_rows(1, 1, range(3))
        load_x(nc.scalar, 0, 2)
        warm = keep.tile([P, 1], F32, name="warm")
        nc.vector.memset(warm[:], 0.0)
        warm_out = keep.tile([P, 1], F32, name="warm_out")
        nc.scalar.copy(out=warm_out[:], in_=warm[:])
        load_words(1, 0)
        load_words(1, 1)
        load_biases(nc.sync, 0, 1)
        load_biases(nc.sync, 1, 0)
        load_biases(nc.sync, 1, 1)
        load_scale_rows(1, 1, range(3, 4))
        load_scale_rows(0, 0, range(2))
        load_words(0, 0)
        load_words(0, 1)
        load_scale_rows(0, 0, range(2, 4))
        load_scale_rows(0, 1, range(4))
        for t in range(4, 8, 2):
            load_x(nc.sync, t, 2)
        for t in range(8, 12, 2):
            load_x(nc.sync, t, 2)
        for t in range(12, TILES, GROUP):
            load_x(nc.sync, t, GROUP)
        nc.gpsimd.memset(gate_rows[:].bitcast(I32), ONES)
        nc.gpsimd.dma_start(out=gate_rows[32:65:32, :], in_=gate_flat.unsqueeze(0).to_broadcast([2, TOKENS]))

        codes = {}
        planes = {}
        blended = {}
        grouped = {}
        sorted_words = {}

        def sort_words(t):
            words = x_sb[:, t, :].bitcast(F32)
            sorted_words[t] = sorted_pool.tile([P, PASSES, 2, P], F32, name="sorted_words")
            nc.scalar.copy(
                out=sorted_words[t][:], in_=words.rearrange("p (g r u) -> p g u r", g=PASSES, u=2)
            )

        def transpose_tiles(tiles):
            for t in tiles:
                xt = psum.tile([P, PASSES, 2, P], F32, name="xt", tag="bank")
                for g in range(PASSES):
                    for u in range(2):
                        if t in sorted_words:
                            nc.tensor.transpose(xt[:, g, u, :], sorted_words[t][:, g, u, :], ident[:])
                        else:
                            words = x_sb[:, t, :].bitcast(F32)
                            nc.tensor.transpose(
                                xt[:, g, u, :], words[:, g * 256 + u : (g + 1) * 256 : 2], ident[:]
                            )
                if t % 2 == 0:
                    grouped[t // 2] = ahead.tile([P, 2, PASSES * P * 4], BF16, name="grouped", align_bytes=256)
                nc.scalar.copy(
                    out=grouped[t // 2][:, t % 2, :].bitcast(F32).rearrange("p (g r u) -> p g r u", g=PASSES, u=2),
                    in_=xt[:].rearrange("p g u r -> p g r u"),
                )

        def quantise_pair(t):
            codes[t // 2] = ahead.tile([P, 2 * PASSES * P], U32, name="codes", align_bytes=256)
            planes[t // 2] = ahead.tile([P, 2 * PASSES * P], U8, name="planes", align_bytes=256)
            nc.vector.quantize_mx(
                out=codes[t // 2][:].bitcast(FP8X4),
                scales=planes[t // 2][:],
                in_=grouped[t // 2][:].rearrange("p j c -> p (j c)"),
            )

        def blend_kind(t):
            if t < len(BLEND_HEAD):
                return BLEND_HEAD[t]
            return BLEND_TAIL[t % GROUP] if t >= TAIL else BLEND_LOOP[t % GROUP]

        def blend_biases(t):
            kind = blend_kind(t)
            if kind == "V":
                blended[t] = biases.tile([P, BANK], F32, name="blended")
                nc.vector.scalar_tensor_tensor(
                    out=blended[t][:], in0=bias_step[:], scalar=m_f[:, t : t + 1], in1=bias_base[:], op0=MULT, op1=ADD
                )
            elif kind == "G":
                step = stage.tile([P, BANK], F32, name="step")
                nc.scalar.activation(out=step[:], in_=bias_step[:], func=COPY, scale=m_f[:, t : t + 1])
                blended[t] = biases.tile([P, BANK], F32, name="blended")
                nc.gpsimd.tensor_tensor(out=blended[t][:], in0=step[:], in1=bias_base[:], op=ADD)
            else:
                blend_ps = psum.tile([P, BANK], F32, name="blend_ps", tag="bank")
                nc.tensor.matmul(
                    out=blend_ps[:],
                    lhsT=gate_rows[:, t * P : (t + 1) * P],
                    rhs=bias_rows[:],
                    start=True,
                    stop=True,
                )
                blended[t] = biases.tile([P, BANK], F32, name="blended")
                nc.scalar.copy(out=blended[t][:], in_=blend_ps[:])

        acc = {}
        parts = {}

        def multiply(t, side):
            acc[t, side] = psum.tile([P, BANK], F32, name="acc%d" % side, tag="bank")
            for g in range(PASSES):
                cols = slice(((t % 2) * PASSES + g) * P, ((t % 2) * PASSES + g + 1) * P)
                nc.tensor.matmul_mx(
                    out=acc[t, side][:],
                    lhsT=codes[t // 2][:, cols].bitcast(FP8X4),
                    lhsT_scale=planes[t // 2][:, cols],
                    rhs=w_words[:, g, side, :].bitcast(FP8X4),
                    rhs_scale=w_planes[side][4 * g : P, :],
                    start=(g == 0),
                    stop=(g == PASSES - 1),
                )

        def reasoning_side(t):
            multiply(t, 1)
            parts[t] = stage.tile([P, BANK], F32, name="part")
            nc.vector.scalar_tensor_tensor(
                out=parts[t][:], in0=acc[t, 1][:], scalar=m_f[:, t : t + 1], in1=blended[t][:], op0=MULT, op1=ADD
            )

        def base_side(t):
            multiply(t, 0)
            result = results.tile([P, BANK], F32, name="result")
            if t % GROUP in G_ENDS and G_FROM <= t < TILES - 2:
                scaled = stage.tile([P, BANK], F32, name="scaled")
                nc.scalar.activation(out=scaled[:], in_=acc[t, 0][:], func=COPY, scale=one_minus_m[:, t : t + 1])
                for half in range(2):
                    cols = slice(half * FEAT, (half + 1) * FEAT)
                    nc.gpsimd.tensor_tensor(out=result[:, cols], in0=scaled[:, cols], in1=parts[t][:, cols], op=ADD)
            else:
                nc.vector.scalar_tensor_tensor(
                    out=result[:], in0=acc[t, 0][:], scalar=one_minus_m[:, t : t + 1], in1=parts[t][:], op0=MULT, op1=ADD
                )
            for half in range(2):
                nc.sync.dma_start(out=out_views[half][:, t, :], in_=result[:, half * FEAT : (half + 1) * FEAT])

        def pair(t):
            for j in (t, t + 1):
                if j + BLENDS_AHEAD < TILES and blend_kind(j + BLENDS_AHEAD) == "P":
                    blend_biases(j + BLENDS_AHEAD)
            for j in (t, t + 1):
                reasoning_side(j)
            if t + QLEAD < TILES:
                quantise_pair(t + QLEAD)
            for j in (t, t + 1):
                base_side(j)
            for j in (t, t + 1):
                if j + BLENDS_AHEAD < TILES and blend_kind(j + BLENDS_AHEAD) != "P":
                    blend_biases(j + BLENDS_AHEAD)

        transpose_tiles(RUNS[0])
        nc.vector.tensor_copy(out=gate_by_tile[0:TILES, :], in_=gate_by_tile_bf[:])
        gate_ps = psum.tile([P, P], F32, name="gate_ps", tag="bank")
        nc.tensor.transpose(gate_ps[:], gate_by_tile[:], ident[:])
        m_f = keep.tile([P, TILES], F32, name="m_f")
        nc.vector.tensor_copy(out=m_f[:], in_=gate_ps[:, 0:TILES])
        one_minus_m = keep.tile([P, TILES], F32, name="one_minus_m")
        nc.vector.tensor_scalar(out=one_minus_m[:], in0=m_f[:], scalar1=-1.0, scalar2=1.0, op0=MULT, op1=ADD)

        base_ps = psum.tile([P, BANK], F32, name="base_ps", tag="bank")
        nc.tensor.matmul(out=base_ps[:], lhsT=pick[:, 0:P], rhs=bias_rows[:], start=True, stop=True)
        bias_base = keep.tile([P, BANK], F32, name="bias_base")
        nc.scalar.copy(out=bias_base[:], in_=base_ps[:])
        bias_step = keep_psum.tile([P, BANK], F32, name="bias_step")
        nc.tensor.matmul(out=bias_step[:], lhsT=pick[:, P : 2 * P], rhs=bias_rows[:], start=True, stop=True)

        quantise_pair(0)
        blend_biases(0)
        blend_biases(1)
        for t in range(2):
            reasoning_side(t)
        transpose_tiles(RUNS[1])
        nc.scalar.activation(out=bias_rows[64:96, :], in_=bias_rows[64:96, :], func=COPY, scale=-1.0)
        quantise_pair(2)
        blend_biases(2)
        blend_biases(3)
        for t in range(2):
            base_side(t)
            blend_biases(t + 4)
        for t in range(2, 4):
            reasoning_side(t)
        transpose_tiles(range(4, 6))
        for t in range(2, 4):
            base_side(t)
        quantise_pair(4)
        transpose_tiles(range(6, 8))
        for t in range(2, 4):
            blend_biases(t + 4)
        quantise_pair(6)
        transpose_tiles(range(8, 10))
        for t in range(GROUP, TILES, 2):
            for j in (t, t + 1):
                if j + SLEAD < TILES:
                    sort_words(j + SLEAD)
            pair(t)
            if t + TLEAD < TILES:
                transpose_tiles(range(t + TLEAD, t + TLEAD + 2))
